import numpy as np
import ml_dtypes

BF16 = ml_dtypes.bfloat16


def bf(x):
    return np.asarray(x, np.float32).astype(BF16)


def f32(x):
    return np.asarray(x, np.float32)


def f64(x):
    return np.asarray(x).astype(np.float64)


def striped(idx):
    return np.tile(idx.reshape(-1, 16).T, (8, 1))


V, D, NH, DH, B, T, N = 4096, 512, 4, 128, 4, 512, 2048
EPS = 1e-6


def pos_encoding():
    pos = np.arange(T, dtype=np.float64)[None, :]
    i = np.arange(D, dtype=np.float64)[:, None]
    ang = pos / np.power(10000.0, 2.0 * (i // 2) / D)
    return np.where((np.arange(D) % 2 == 0)[:, None], np.sin(ang), np.cos(ang))


def setup_inputs():
    sc = 1.0 / np.sqrt(D)
    return {
        "emb": f32(sc * np.random.standard_normal((D, V))),
        "pe": f32(pos_encoding()),
        "wq": bf(sc * np.random.standard_normal((D, D))),
        "bq": f32(0.5 * np.random.standard_normal((D, 1))),
        "wk": bf(sc * np.random.standard_normal((D, D))),
        "wv": bf(sc * np.random.standard_normal((D, D))),
        "bv": f32(0.1 * np.random.standard_normal((D, 1))),
        "wo": bf(sc * np.random.standard_normal((D, D))),
        "bo": f32(0.1 * np.random.standard_normal((D, 1))),
        "gain": f32(1.0 + 0.1 * np.random.standard_normal((D, 1))),
        "shift": f32(0.1 * np.random.standard_normal((D, 1))),
        "offs": striped(np.random.permutation(np.tile(np.arange(V), 2))[:N]),
    }


def reference(emb, pe, wq, bq, wk, wv, bv, wo, bo, gain, shift, offs):
    idx = offs[:16].T.reshape(-1)
    x0 = np.sqrt(D) * f64(emb)[:, idx] + np.tile(f64(pe), (1, B))
    q = f64(wq).T @ x0 + f64(bq)
    k = f64(wk).T @ x0
    v = f64(wv).T @ x0 + f64(bv)
    av = np.zeros((D, N))
    for n in range(B):
        cols = slice(n * T, (n + 1) * T)
        for h in range(NH):
            rows = slice(h * DH, (h + 1) * DH)
            s = q[rows, cols].T @ k[rows, cols] / np.sqrt(DH)
            e = np.exp(s - s.max(axis=1, keepdims=True))
            a = e / e.sum(axis=1, keepdims=True)
            av[rows, cols] = v[rows, cols] @ a.T
    y = x0 + f64(wo).T @ av + f64(bo)
    m = y.mean(axis=0, keepdims=True)
    var = np.square(y - m).mean(axis=0, keepdims=True)
    return f64(gain) * (y - m) / np.sqrt(var + EPS) + f64(shift)

@@ -1,0 +1,205 @@
+import math
+
+import concourse.mybir as mybir
+from concourse.masks import make_identity
+
+F32 = mybir.dt.float32
+BF16 = mybir.dt.bfloat16
+U16 = mybir.dt.uint16
+ALU = mybir.AluOpType
+ACT = mybir.ActivationFunctionType
+AX = mybir.AxisListType
+
+P = 128
+V = 4096
+D = 512
+NH = 4
+B = 4
+T = 512
+CB = D // P
+TB = T // P
+EPS = 1e-6
+EMB_SCALE = math.sqrt(D)
+
+FLOPS = 2 * D * D * B * T * 4 + 2 * 2 * B * NH * T * T * P
+
+
+def tile_texttransformer_b_kernel(
+    tc, emb, pe, wq, bq, wk, wv, bv, wo, bo, gain, shift, offs, out
+):
+    nc = tc.nc
+    with (
+        tc.tile_pool(name="held", bufs=1) as held,
+        tc.tile_pool(name="seq", bufs=2) as seq,
+        tc.tile_pool(name="work", bufs=4) as work,
+        tc.psum_pool(name="psum", bufs=1) as psum,
+    ):
+        offsets = held.tile([P, B * T // 16], U16, name="offsets")
+        nc.sync.dma_start(offsets[:], offs)
+
+        pe_sb = held.tile([P, CB, T], F32, name="pe_sb")
+        table = [held.tile([P, V], F32, name=f"table{c}") for c in range(CB)]
+        for c in range(CB):
+            rows_c = slice(c * P, (c + 1) * P)
+            nc.sync.dma_start(pe_sb[:, c, :], pe[rows_c, :])
+            nc.scalar.mul(pe_sb[:, c, :], pe_sb[:, c, :], 1.0 / EMB_SCALE)
+            for half in range(2):
+                cols_h = slice(half * V // 2, (half + 1) * V // 2)
+                nc.sync.dma_start(table[c][:, cols_h], emb[rows_c, cols_h])
+
+        weights = {}
+        for name, w in (("q", wq), ("k", wk), ("v", wv), ("o", wo)):
+            weights[name] = held.tile([P, CB, D], BF16, name=f"w{name}")
+            nc.gpsimd.dma_start(weights[name][:], w.rearrange("(c p) e -> p c e", p=P))
+
+        vec_rows = held.tile([P, P], F32, name="vec_rows")
+        nc.vector.memset(vec_rows[:], 0.0)
+        for v, vec in enumerate((bq, bv, bo, gain, shift)):
+            nc.gpsimd.dma_start(
+                vec_rows[v * CB : (v + 1) * CB, :], vec.rearrange("(b p) o -> b (p o)", p=P)
+            )
+        ident_f = held.tile([P, P], F32, name="ident_f")
+        make_identity(nc, ident_f[:])
+        ident_b = held.tile([P, P], BF16, name="ident_b")
+        make_identity(nc, ident_b[:])
+        vec_ps = psum.tile([P, P], F32, name="vec_ps", tag="acc", bufs=6)
+        nc.tensor.transpose(vec_ps[:], vec_rows[:], ident_f[:])
+        vec_cols = held.tile([P, 5 * CB], F32, name="vec_cols")
+        nc.vector.tensor_copy(vec_cols[:], vec_ps[:, 0 : 5 * CB])
+
+        def column(v, b):
+            return vec_cols[:, v * CB + b : v * CB + b + 1]
+
+        mean_w = held.tile([P, P], BF16, name="mean_w")
+        nc.vector.memset(mean_w[:], 1.0 / D)
+        eps_col = held.tile([P, 1], F32, name="eps_col")
+        nc.vector.memset(eps_col[:], EPS)
+
+        x0 = [held.tile([P, CB, T], F32, name=f"x0_{n}") for n in range(B)]
+        x0b = [held.tile([P, CB, T], BF16, name=f"x0b_{n}") for n in range(B)]
+        for c in range(CB):
+            for n in range(B):
+                piece = offsets[:, n * T // 16 : (n + 1) * T // 16]
+                nc.vector.tensor_tensor(
+                    x0[n][:, c, :], table[c][:].indirect(piece), pe_sb[:, c, :], ALU.add
+                )
+                nc.gpsimd.tensor_scalar(
+                    x0b[n][:, c, :], x0[n][:, c, :], EMB_SCALE, 0.0, ALU.mult, ALU.add
+                )
+
+        def project(n):
+            q = seq.tile([P, NH, T], BF16, name="q")
+            k = seq.tile([P, NH, T], BF16, name="k")
+            vT = seq.tile([P, TB, D], BF16, name="vT")
+            for h in range(NH):
+                head = slice(h * P, (h + 1) * P)
+                q_ps = psum.tile([P, T], F32, name="q_ps", tag="acc", bufs=6)
+                for c in range(CB):
+                    nc.tensor.matmul(
+                        q_ps[:], weights["q"][:, c, head], x0b[n][:, c, :],
+                        start=c == 0, stop=c == CB - 1,
+                    )
+                nc.vector.tensor_scalar(
+                    q[:, h, :], q_ps[:], column(0, h), 1.0 / math.sqrt(P), ALU.add, ALU.mult
+                )
+                k_ps = psum.tile([P, T], F32, name="k_ps", tag="acc", bufs=6)
+                for c in range(CB):
+                    nc.tensor.matmul(
+                        k_ps[:], weights["k"][:, c, head], x0b[n][:, c, :],
+                        start=c == 0, stop=c == CB - 1,
+                    )
+                nc.any.tensor_copy(k[:, h, :], k_ps[:])
+            for ub in range(TB):
+                v_ps = psum.tile([P, D], F32, name="v_ps", tag="acc", bufs=6)
+                for c in range(CB):
+                    nc.tensor.matmul(
+                        v_ps[:], x0b[n][:, c, ub * P : (ub + 1) * P], weights["v"][:, c, :],
+                        start=c == 0, stop=c == CB - 1,
+                    )
+                nc.any.tensor_copy(vT[:, ub, :], v_ps[:])
+            return q, k, vT
+
+        def attend(q, k, vT):
+            av = seq.tile([P, NH, T], BF16, name="av")
+            for h in range(NH):
+                aT = work.tile([P, TB, T], BF16, name="aT", bufs=2)
+                for tb in range(TB):
+                    rows_t = slice(tb * P, (tb + 1) * P)
+                    s_ps = psum.tile([P, T], F32, name="s_ps", tag="acc", bufs=6)
+                    nc.tensor.matmul(s_ps[:], q[:, h, rows_t], k[:, h, :], start=True, stop=True)
+                    neg_max = work.tile([P, 1], F32, name="neg_max")
+                    nc.vector.reduce_max(neg_max[:], s_ps[:], axis=AX.X, negate=True)
+                    e = work.tile([P, T], BF16, name="e")
+                    e_sum = work.tile([P, 1], F32, name="e_sum")
+                    nc.scalar.activation(
+                        e[:], s_ps[:], ACT.Exp, bias=neg_max[:], scale=1.0, accum_out=e_sum[:]
+                    )
+                    recip = work.tile([P, 1], F32, name="recip")
+                    nc.vector.reciprocal(recip[:], e_sum[:])
+                    diag = work.tile([P, P], BF16, name="diag")
+                    nc.vector.tensor_scalar_mul(diag[:], ident_b[:], recip[:])
+                    aT_ps = psum.tile([P, TB, P], BF16, name="aT_ps", tag="aT", bufs=2)
+                    for ub in range(TB):
+                        nc.tensor.matmul(
+                            aT_ps[:, ub, :], e[:, ub * P : (ub + 1) * P], diag[:],
+                            start=True, stop=True,
+                        )
+                    nc.any.tensor_copy(aT[:, :, rows_t], aT_ps[:])
+                av_ps = psum.tile([P, T], F32, name="av_ps", tag="acc", bufs=6)
+                for ub in range(TB):
+                    nc.tensor.matmul(
+                        av_ps[:], vT[:, ub, h * P : (h + 1) * P], aT[:, ub, :],
+                        start=ub == 0, stop=ub == TB - 1,
+                    )
+                nc.scalar.activation(av[:, h, :], av_ps[:], ACT.Identity, bias=column(1, h))
+            return av
+
+        def finish(n, av):
+            y = x0[n]
+            yb = seq.tile([P, CB, T], BF16, name="yb")
+            for eb in range(CB):
+                y_ps = psum.tile([P, T], F32, name="y_ps", tag="acc", bufs=6)
+                for h in range(NH):
+                    nc.tensor.matmul(
+                        y_ps[:], weights["o"][:, h, eb * P : (eb + 1) * P], av[:, h, :],
+                        start=h == 0, stop=h == NH - 1,
+                    )
+                nc.vector.scalar_tensor_tensor(
+                    y[:, eb, :], y[:, eb, :], EMB_SCALE, y_ps[:], ALU.mult, ALU.add
+                )
+                nc.gpsimd.tensor_scalar(
+                    yb[:, eb, :], y[:, eb, :], column(2, eb), 1.0, ALU.add, ALU.mult
+                )
+            mean_ps = psum.tile([P, T], F32, name="mean_ps", tag="acc", bufs=6)
+            for eb in range(CB):
+                nc.tensor.matmul(
+                    mean_ps[:], mean_w[:], yb[:, eb, :], start=eb == 0, stop=eb == CB - 1
+                )
+            sq = seq.tile([P, CB, T], BF16, name="sq")
+            for eb in range(CB):
+                nc.vector.scalar_tensor_tensor(
+                    y[:, eb, :], y[:, eb, :], column(2, eb), mean_ps[:], ALU.add, ALU.subtract
+                )
+                nc.scalar.activation(sq[:, eb, :], y[:, eb, :], ACT.Square)
+            var_ps = psum.tile([P, T], F32, name="var_ps", tag="acc", bufs=6)
+            for eb in range(CB):
+                nc.tensor.matmul(
+                    var_ps[:], mean_w[:], sq[:, eb, :], start=eb == 0, stop=eb == CB - 1
+                )
+            log_var = seq.tile([P, T], F32, name="log_var")
+            nc.scalar.activation(log_var[:], var_ps[:], ACT.Ln, bias=eps_col[:])
+            rstd = seq.tile([P, T], F32, name="rstd")
+            nc.scalar.activation(rstd[:], log_var[:], ACT.Exp, scale=-0.5)
+            for eb in range(CB):
+                nc.vector.tensor_tensor(y[:, eb, :], y[:, eb, :], rstd[:], ALU.mult)
+                nc.vector.tensor_scalar(
+                    y[:, eb, :], y[:, eb, :], column(3, eb), column(4, eb), ALU.mult, ALU.add
+                )
+                nc.sync.dma_start(out[eb * P : (eb + 1) * P, n * T : (n + 1) * T], y[:, eb, :])
+
+        qkv = project(0)
+        for n in range(B):
+            av = attend(*qkv)
+            if n + 1 < B:
+                qkv = project(n + 1)
+            finish(n, av)

@@ -18,10 +18,29 @@ B = 4
 T = 512
 CB = D // P
 TB = T // P
+BANKS = 8
 EPS = 1e-6
 EMB_SCALE = math.sqrt(D)
 
 FLOPS = 2 * D * D * B * T * 4 + 2 * 2 * B * NH * T * T * P
+
+GROUPS = (
+    [(kind, g) for g in (0, 1) for kind in ("q", "k")]
+    + [("v", g) for g in range(TB)]
+    + [(kind, g) for g in (2, 3) for kind in ("q", "k")]
+)
+
+DIAG_LAG = 1
+TURN_LAG = 2
+SUM_LAG = 3
+BLOCKS = NH * TB
+
+
+def alternate(first, second):
+    merged = []
+    for i in range(max(len(first), len(second))):
+        merged += first[i : i + 1] + second[i : i + 1]
+    return merged
 
 
 def tile_texttransformer_b_kernel(
@@ -32,7 +51,7 @@ def tile_texttransformer_b_kernel(
         tc.tile_pool(name="held", bufs=1) as held,
         tc.tile_pool(name="seq", bufs=2) as seq,
         tc.tile_pool(name="work", bufs=4) as work,
-        tc.psum_pool(name="psum", bufs=1) as psum,
+        tc.psum_pool(name="psum", bufs=BANKS) as psum,
     ):
         offsets = held.tile([P, B * T // 16], U16, name="offsets")
         nc.sync.dma_start(offsets[:], offs)
@@ -47,22 +66,22 @@ def tile_texttransformer_b_kernel(
                 cols_h = slice(half * V // 2, (half + 1) * V // 2)
                 nc.sync.dma_start(table[c][:, cols_h], emb[rows_c, cols_h])
 
-        weights = {}
-        for name, w in (("q", wq), ("k", wk), ("v", wv), ("o", wo)):
-            weights[name] = held.tile([P, CB, D], BF16, name=f"w{name}")
-            nc.gpsimd.dma_start(weights[name][:], w.rearrange("(c p) e -> p c e", p=P))
-
         vec_rows = held.tile([P, P], F32, name="vec_rows")
         nc.vector.memset(vec_rows[:], 0.0)
         for v, vec in enumerate((bq, bv, bo, gain, shift)):
             nc.gpsimd.dma_start(
                 vec_rows[v * CB : (v + 1) * CB, :], vec.rearrange("(b p) o -> b (p o)", p=P)
             )
+        weights = {}
+        for name, w in (("q", wq), ("k", wk), ("v", wv), ("o", wo)):
+            weights[name] = held.tile([P, CB, D], BF16, name=f"w{name}")
+            nc.gpsimd.dma_start(weights[name][:], w.rearrange("(c p) e -> p c e", p=P))
+
         ident_f = held.tile([P, P], F32, name="ident_f")
         make_identity(nc, ident_f[:])
         ident_b = held.tile([P, P], BF16, name="ident_b")
         make_identity(nc, ident_b[:])
-        vec_ps = psum.tile([P, P], F32, name="vec_ps", tag="acc", bufs=6)
+        vec_ps = psum.tile([P, P], F32, name="vec_ps", tag="bank")
         nc.tensor.transpose(vec_ps[:], vec_rows[:], ident_f[:])
         vec_cols = held.tile([P, 5 * CB], F32, name="vec_cols")
         nc.vector.tensor_copy(vec_cols[:], vec_ps[:, 0 : 5 * CB])
@@ -77,114 +96,135 @@ def tile_texttransformer_b_kernel(
 
         x0 = [held.tile([P, CB, T], F32, name=f"x0_{n}") for n in range(B)]
         x0b = [held.tile([P, CB, T], BF16, name=f"x0b_{n}") for n in range(B)]
-        for c in range(CB):
-            for n in range(B):
-                piece = offsets[:, n * T // 16 : (n + 1) * T // 16]
-                nc.vector.tensor_tensor(
-                    x0[n][:, c, :], table[c][:].indirect(piece), pe_sb[:, c, :], ALU.add
-                )
-                nc.gpsimd.tensor_scalar(
-                    x0b[n][:, c, :], x0[n][:, c, :], EMB_SCALE, 0.0, ALU.mult, ALU.add
-                )
 
-        def project(n):
-            q = seq.tile([P, NH, T], BF16, name="q")
-            k = seq.tile([P, NH, T], BF16, name="k")
-            vT = seq.tile([P, TB, D], BF16, name="vT")
-            for h in range(NH):
-                head = slice(h * P, (h + 1) * P)
-                q_ps = psum.tile([P, T], F32, name="q_ps", tag="acc", bufs=6)
-                for c in range(CB):
-                    nc.tensor.matmul(
-                        q_ps[:], weights["q"][:, c, head], x0b[n][:, c, :],
-                        start=c == 0, stop=c == CB - 1,
-                    )
+        def look_up(c, n):
+            piece = offsets[:, n * T // 16 : (n + 1) * T // 16]
+            nc.vector.tensor_tensor(
+                x0[n][:, c, :], table[c][:].indirect(piece), pe_sb[:, c, :], ALU.add
+            )
+            nc.gpsimd.tensor_scalar(
+                x0b[n][:, c, :], x0[n][:, c, :], EMB_SCALE, 0.0, ALU.mult, ALU.add
+            )
+
+        qkv = {}
+
+        def new_qkv(n):
+            qkv[n] = {kind: seq.tile([P, NH, T], BF16, name=kind) for kind in ("q", "k", "v")}
+
+        def project_matmul(ps, n, kind, g, c):
+            block = slice(g * P, (g + 1) * P)
+            if kind == "v":
+                lhsT, rhs = x0b[n][:, c, block], weights["v"][:, c, :]
+            else:
+                lhsT, rhs = weights[kind][:, c, block], x0b[n][:, c, :]
+            nc.tensor.matmul(ps[:], lhsT, rhs, start=c == 0, stop=c == CB - 1)
+
+        def project_out(ps, n, kind, g):
+            dest = qkv[n][kind][:, g, :]
+            if kind == "q":
                 nc.vector.tensor_scalar(
-                    q[:, h, :], q_ps[:], column(0, h), 1.0 / math.sqrt(P), ALU.add, ALU.mult
+                    dest, ps[:], column(0, g), 1.0 / math.sqrt(P), ALU.add, ALU.mult
                 )
-                k_ps = psum.tile([P, T], F32, name="k_ps", tag="acc", bufs=6)
-                for c in range(CB):
-                    nc.tensor.matmul(
-                        k_ps[:], weights["k"][:, c, head], x0b[n][:, c, :],
-                        start=c == 0, stop=c == CB - 1,
-                    )
-                nc.any.tensor_copy(k[:, h, :], k_ps[:])
+            elif kind == "k" or g % 2 == 1:
+                nc.scalar.copy(dest, ps[:])
+            else:
+                nc.vector.tensor_copy(dest, ps[:])
+
+        def project_group(n, kind, g):
+            ps = psum.tile([P, T], F32, name="proj_ps", tag="bank")
+            for c in range(CB):
+                project_matmul(ps, n, kind, g, c)
+            project_out(ps, n, kind, g)
+
+        def scores(n, h, tb):
+            s_ps = psum.tile([P, T], F32, name="s_ps", tag="bank")
+            nc.tensor.matmul(
+                s_ps[:], qkv[n]["q"][:, h, tb * P : (tb + 1) * P], qkv[n]["k"][:, h, :],
+                start=True, stop=True,
+            )
+            neg_max = work.tile([P, 1], F32, name="neg_max")
+            nc.vector.reduce_max(neg_max[:], s_ps[:], axis=AX.X, negate=True)
+            e = work.tile([P, T], BF16, name="e")
+            e_sum = work.tile([P, 1], F32, name="e_sum")
+            nc.scalar.activation(
+                e[:], s_ps[:], ACT.Exp, bias=neg_max[:], scale=1.0, accum_out=e_sum[:]
+            )
+            return {"e": e, "e_sum": e_sum}
+
+        def make_diag(block):
+            recip = work.tile([P, 1], F32, name="recip")
+            nc.vector.reciprocal(recip[:], block["e_sum"][:])
+            block["diag"] = work.tile([P, P], BF16, name="diag")
+            nc.vector.tensor_scalar_mul(block["diag"][:], ident_b[:], recip[:])
+
+        def turn(block, aT, tb):
+            aT_ps = psum.tile([P, TB, P], BF16, name="aT_ps", tag="bank")
             for ub in range(TB):
-                v_ps = psum.tile([P, D], F32, name="v_ps", tag="acc", bufs=6)
-                for c in range(CB):
-                    nc.tensor.matmul(
-                        v_ps[:], x0b[n][:, c, ub * P : (ub + 1) * P], weights["v"][:, c, :],
-                        start=c == 0, stop=c == CB - 1,
-                    )
-                nc.any.tensor_copy(vT[:, ub, :], v_ps[:])
-            return q, k, vT
+                nc.tensor.matmul(
+                    aT_ps[:, ub, :], block["e"][:, ub * P : (ub + 1) * P], block["diag"][:],
+                    start=True, stop=True,
+                )
+            if tb % 2 == 0:
+                nc.vector.tensor_copy(aT[:, :, tb * P : (tb + 1) * P], aT_ps[:])
+            else:
+                nc.scalar.copy(aT[:, :, tb * P : (tb + 1) * P], aT_ps[:])
 
-        def attend(q, k, vT):
-            av = seq.tile([P, NH, T], BF16, name="av")
-            for h in range(NH):
-                aT = work.tile([P, TB, T], BF16, name="aT", bufs=2)
-                for tb in range(TB):
-                    rows_t = slice(tb * P, (tb + 1) * P)
-                    s_ps = psum.tile([P, T], F32, name="s_ps", tag="acc", bufs=6)
-                    nc.tensor.matmul(s_ps[:], q[:, h, rows_t], k[:, h, :], start=True, stop=True)
-                    neg_max = work.tile([P, 1], F32, name="neg_max")
-                    nc.vector.reduce_max(neg_max[:], s_ps[:], axis=AX.X, negate=True)
-                    e = work.tile([P, T], BF16, name="e")
-                    e_sum = work.tile([P, 1], F32, name="e_sum")
-                    nc.scalar.activation(
-                        e[:], s_ps[:], ACT.Exp, bias=neg_max[:], scale=1.0, accum_out=e_sum[:]
-                    )
-                    recip = work.tile([P, 1], F32, name="recip")
-                    nc.vector.reciprocal(recip[:], e_sum[:])
-                    diag = work.tile([P, P], BF16, name="diag")
-                    nc.vector.tensor_scalar_mul(diag[:], ident_b[:], recip[:])
-                    aT_ps = psum.tile([P, TB, P], BF16, name="aT_ps", tag="aT", bufs=2)
-                    for ub in range(TB):
-                        nc.tensor.matmul(
-                            aT_ps[:, ub, :], e[:, ub * P : (ub + 1) * P], diag[:],
-                            start=True, stop=True,
-                        )
-                    nc.any.tensor_copy(aT[:, :, rows_t], aT_ps[:])
-                av_ps = psum.tile([P, T], F32, name="av_ps", tag="acc", bufs=6)
-                for ub in range(TB):
-                    nc.tensor.matmul(
-                        av_ps[:], vT[:, ub, h * P : (h + 1) * P], aT[:, ub, :],
-                        start=ub == 0, stop=ub == TB - 1,
-                    )
-                nc.scalar.activation(av[:, h, :], av_ps[:], ACT.Identity, bias=column(1, h))
-            return av
+        av = {}
 
-        def finish(n, av):
+        def weighted_sum(n, h, aT):
+            if h == 0:
+                av[n] = seq.tile([P, NH, T], BF16, name="av")
+            av_ps = psum.tile([P, T], F32, name="av_ps", tag="bank")
+            for ub in range(TB):
+                nc.tensor.matmul(
+                    av_ps[:], qkv[n]["v"][:, ub, h * P : (h + 1) * P], aT[:, ub, :],
+                    start=ub == 0, stop=ub == TB - 1,
+                )
+            nc.scalar.activation(av[n][:, h, :], av_ps[:], ACT.Identity, bias=column(1, h))
+
+        norm = {}
+
+        def wo_step(n, eb):
             y = x0[n]
-            yb = seq.tile([P, CB, T], BF16, name="yb")
-            for eb in range(CB):
-                y_ps = psum.tile([P, T], F32, name="y_ps", tag="acc", bufs=6)
-                for h in range(NH):
-                    nc.tensor.matmul(
-                        y_ps[:], weights["o"][:, h, eb * P : (eb + 1) * P], av[:, h, :],
-                        start=h == 0, stop=h == NH - 1,
-                    )
-                nc.vector.scalar_tensor_tensor(
-                    y[:, eb, :], y[:, eb, :], EMB_SCALE, y_ps[:], ALU.mult, ALU.add
+            if eb == 0:
+                norm[n] = {name: seq.tile([P, CB, T], BF16, name=name) for name in ("yb", "sq")}
+            y_ps = psum.tile([P, T], F32, name="y_ps", tag="bank")
+            for h in range(NH):
+                nc.tensor.matmul(
+                    y_ps[:], weights["o"][:, h, eb * P : (eb + 1) * P], av[n][:, h, :],
+                    start=h == 0, stop=h == NH - 1,
                 )
-                nc.gpsimd.tensor_scalar(
-                    yb[:, eb, :], y[:, eb, :], column(2, eb), 1.0, ALU.add, ALU.mult
-                )
-            mean_ps = psum.tile([P, T], F32, name="mean_ps", tag="acc", bufs=6)
+            nc.vector.scalar_tensor_tensor(
+                y[:, eb, :], y[:, eb, :], EMB_SCALE, y_ps[:], ALU.mult, ALU.add
+            )
+            nc.gpsimd.tensor_scalar(
+                norm[n]["yb"][:, eb, :], y[:, eb, :], column(2, eb), 1.0, ALU.add, ALU.mult
+            )
+
+        def mean_step(n):
+            y = x0[n]
+            mean_ps = psum.tile([P, T], F32, name="mean_ps", tag="bank")
             for eb in range(CB):
                 nc.tensor.matmul(
-                    mean_ps[:], mean_w[:], yb[:, eb, :], start=eb == 0, stop=eb == CB - 1
+                    mean_ps[:], mean_w[:], norm[n]["yb"][:, eb, :],
+                    start=eb == 0, stop=eb == CB - 1,
                 )
-            sq = seq.tile([P, CB, T], BF16, name="sq")
             for eb in range(CB):
                 nc.vector.scalar_tensor_tensor(
                     y[:, eb, :], y[:, eb, :], column(2, eb), mean_ps[:], ALU.add, ALU.subtract
                 )
-                nc.scalar.activation(sq[:, eb, :], y[:, eb, :], ACT.Square)
-            var_ps = psum.tile([P, T], F32, name="var_ps", tag="acc", bufs=6)
+                nc.scalar.activation(norm[n]["sq"][:, eb, :], y[:, eb, :], ACT.Square)
+
+        def no_step():
+            pass
+
+        def var_step(n):
+            y = x0[n]
+            var_ps = psum.tile([P, T], F32, name="var_ps", tag="bank")
             for eb in range(CB):
                 nc.tensor.matmul(
-                    var_ps[:], mean_w[:], sq[:, eb, :], start=eb == 0, stop=eb == CB - 1
+                    var_ps[:], mean_w[:], norm[n]["sq"][:, eb, :],
+                    start=eb == 0, stop=eb == CB - 1,
                 )
             log_var = seq.tile([P, T], F32, name="log_var")
             nc.scalar.activation(log_var[:], var_ps[:], ACT.Ln, bias=eps_col[:])
@@ -192,14 +232,63 @@ def tile_texttransformer_b_kernel(
             nc.scalar.activation(rstd[:], log_var[:], ACT.Exp, scale=-0.5)
             for eb in range(CB):
                 nc.vector.tensor_tensor(y[:, eb, :], y[:, eb, :], rstd[:], ALU.mult)
-                nc.vector.tensor_scalar(
+                nc.gpsimd.tensor_scalar(
                     y[:, eb, :], y[:, eb, :], column(3, eb), column(4, eb), ALU.mult, ALU.add
                 )
                 nc.sync.dma_start(out[eb * P : (eb + 1) * P, n * T : (n + 1) * T], y[:, eb, :])
 
-        qkv = project(0)
-        for n in range(B):
-            av = attend(*qkv)
+        def finish_steps(n):
+            return (
+                [(wo_step, (n, eb)) for eb in range(CB)]
+                + [(mean_step, (n,)), (no_step, ()), (var_step, (n,))]
+            )
+
+        def side_steps(n):
+            ahead = []
+            if n == 0:
+                ahead += [(project_group, (0, kind, g)) for kind, g in GROUPS[BANKS:]]
             if n + 1 < B:
-                qkv = project(n + 1)
-            finish(n, av)
+                new_qkv(n + 1)
+                ahead += [(project_group, (n + 1, kind, g)) for kind, g in GROUPS]
+            behind = finish_steps(n - 1) if n > 0 else []
+            lead = (ahead + [(no_step, ())] * (SUM_LAG + 1))[: SUM_LAG + 1]
+            return lead + alternate(behind, ahead[SUM_LAG + 1 :])
+
+        new_qkv(0)
+        first_ps = [psum.tile([P, T], F32, name=f"first_ps{i}", tag="bank") for i in range(BANKS)]
+        for c in range(CB):
+            for n in range(B if c < CB - 1 else 1):
+                look_up(c, n)
+            for ps, (kind, g) in zip(first_ps, GROUPS):
+                project_matmul(ps, 0, kind, g, c)
+        for ps, (kind, g) in zip(first_ps, GROUPS):
+            project_out(ps, 0, kind, g)
+
+        blocks = [(n, h, tb) for n in range(B) for h in range(NH) for tb in range(TB)]
+        soft = {}
+        aT = {}
+        for i in range(len(blocks) + SUM_LAG):
+            if i < len(blocks):
+                n, h, tb = blocks[i]
+                soft[i] = scores(n, h, tb)
+            if 0 <= i - DIAG_LAG < len(blocks):
+                make_diag(soft[i - DIAG_LAG])
+            if i < len(blocks):
+                j = i % BLOCKS
+                if j == 0:
+                    steps = side_steps(n)
+                    if n + 1 < B:
+                        look_up(CB - 1, n + 1)
+                for step, args in steps[len(steps) * j // BLOCKS : len(steps) * (j + 1) // BLOCKS]:
+                    step(*args)
+            if 0 <= i - TURN_LAG < len(blocks):
+                n2, h2, tb2 = blocks[i - TURN_LAG]
+                if tb2 == 0:
+                    aT[n2, h2] = work.tile([P, TB, T], BF16, name="aT", bufs=2)
+                turn(soft[i - TURN_LAG], aT[n2, h2], tb2)
+            if 0 <= i - SUM_LAG:
+                n3, h3, tb3 = blocks[i - SUM_LAG]
+                if tb3 == TB - 1:
+                    weighted_sum(n3, h3, aT[n3, h3])
+        for step, args in finish_steps(B - 1):
+            step(*args)

@@ -160,10 +160,11 @@ def tile_texttransformer_b_kernel(
         def turn(block, aT, tb):
             aT_ps = psum.tile([P, TB, P], BF16, name="aT_ps", tag="bank")
             for ub in range(TB):
-                nc.tensor.matmul(
-                    aT_ps[:, ub, :], block["e"][:, ub * P : (ub + 1) * P], block["diag"][:],
-                    start=True, stop=True,
-                )
+                for again in range(2):
+                    nc.tensor.matmul(
+                        aT_ps[:, ub, :], block["e"][:, ub * P : (ub + 1) * P], block["diag"][:],
+                        start=True, stop=True,
+                    )
             if tb % 2 == 0:
                 nc.vector.tensor_copy(aT[:, :, tb * P : (tb + 1) * P], aT_ps[:])
             else:

@@ -30,17 +30,7 @@ GROUPS = (
     + [(kind, g) for g in (2, 3) for kind in ("q", "k")]
 )
 
-DIAG_LAG = 1
-TURN_LAG = 2
-SUM_LAG = 3
 BLOCKS = NH * TB
-
-
-def alternate(first, second):
-    merged = []
-    for i in range(max(len(first), len(second))):
-        merged += first[i : i + 1] + second[i : i + 1]
-    return merged
 
 
 def tile_texttransformer_b_kernel(
@@ -50,11 +40,23 @@ def tile_texttransformer_b_kernel(
     with (
         tc.tile_pool(name="held", bufs=1) as held,
         tc.tile_pool(name="seq", bufs=2) as seq,
-        tc.tile_pool(name="work", bufs=4) as work,
+        tc.tile_pool(name="work", bufs=3) as work,
         tc.psum_pool(name="psum", bufs=BANKS) as psum,
     ):
         offsets = held.tile([P, B * T // 16], U16, name="offsets")
         nc.sync.dma_start(offsets[:], offs)
+
+        vec_rows = held.tile([P, P], F32, name="vec_rows")
+        nc.vector.memset(vec_rows[:], 0.0)
+        for v, vec in enumerate((bq, bv, bo, gain, shift)):
+            nc.sync.dma_start(
+                vec_rows[v * CB : (v + 1) * CB, :], vec.rearrange("(b p) o -> b (p o)", p=P)
+            )
+
+        weights = {name: held.tile([P, CB, D], BF16, name=f"w{name}") for name in "qkvo"}
+
+        def load_weights(name, w):
+            nc.sync.dma_start(weights[name][:], w.rearrange("(c p) e -> p c e", p=P))
 
         pe_sb = held.tile([P, CB, T], F32, name="pe_sb")
         table = [held.tile([P, V], F32, name=f"table{c}") for c in range(CB)]
@@ -65,17 +67,11 @@ def tile_texttransformer_b_kernel(
             for half in range(2):
                 cols_h = slice(half * V // 2, (half + 1) * V // 2)
                 nc.sync.dma_start(table[c][:, cols_h], emb[rows_c, cols_h])
-
-        vec_rows = held.tile([P, P], F32, name="vec_rows")
-        nc.vector.memset(vec_rows[:], 0.0)
-        for v, vec in enumerate((bq, bv, bo, gain, shift)):
-            nc.gpsimd.dma_start(
-                vec_rows[v * CB : (v + 1) * CB, :], vec.rearrange("(b p) o -> b (p o)", p=P)
-            )
-        weights = {}
-        for name, w in (("q", wq), ("k", wk), ("v", wv), ("o", wo)):
-            weights[name] = held.tile([P, CB, D], BF16, name=f"w{name}")
-            nc.gpsimd.dma_start(weights[name][:], w.rearrange("(c p) e -> p c e", p=P))
+            if c == 0:
+                load_weights("q", wq)
+                load_weights("k", wk)
+                load_weights("v", wv)
+        load_weights("o", wo)
 
         ident_f = held.tile([P, P], F32, name="ident_f")
         make_identity(nc, ident_f[:])
@@ -125,10 +121,8 @@ def tile_texttransformer_b_kernel(
                 nc.vector.tensor_scalar(
                     dest, ps[:], column(0, g), 1.0 / math.sqrt(P), ALU.add, ALU.mult
                 )
-            elif kind == "k" or g % 2 == 1:
-                nc.scalar.copy(dest, ps[:])
             else:
-                nc.vector.tensor_copy(dest, ps[:])
+                nc.scalar.copy(dest, ps[:])
 
         def project_group(n, kind, g):
             ps = psum.tile([P, T], F32, name="proj_ps", tag="bank")
@@ -136,49 +130,58 @@ def tile_texttransformer_b_kernel(
                 project_matmul(ps, n, kind, g, c)
             project_out(ps, n, kind, g)
 
-        def scores(n, h, tb):
+        def new_head():
+            return {
+                "neg_max": work.tile([P, TB], F32, name="neg_max"),
+                "e": work.tile([P, TB, T], BF16, name="e"),
+                "e_sum": work.tile([P, TB], F32, name="e_sum"),
+            }
+
+        def scores(head, n, h, tb):
             s_ps = psum.tile([P, T], F32, name="s_ps", tag="bank")
             nc.tensor.matmul(
                 s_ps[:], qkv[n]["q"][:, h, tb * P : (tb + 1) * P], qkv[n]["k"][:, h, :],
                 start=True, stop=True,
             )
-            neg_max = work.tile([P, 1], F32, name="neg_max")
-            nc.vector.reduce_max(neg_max[:], s_ps[:], axis=AX.X, negate=True)
-            e = work.tile([P, T], BF16, name="e")
-            e_sum = work.tile([P, 1], F32, name="e_sum")
+            neg_max = head["neg_max"][:, tb : tb + 1]
+            nc.vector.reduce_max(neg_max, s_ps[:], axis=AX.X, negate=True)
             nc.scalar.activation(
-                e[:], s_ps[:], ACT.Exp, bias=neg_max[:], scale=1.0, accum_out=e_sum[:]
+                head["e"][:, tb, :], s_ps[:], ACT.Exp, bias=neg_max, scale=1.0,
+                accum_out=head["e_sum"][:, tb : tb + 1],
             )
-            return {"e": e, "e_sum": e_sum}
 
-        def make_diag(block):
-            recip = work.tile([P, 1], F32, name="recip")
-            nc.vector.reciprocal(recip[:], block["e_sum"][:])
-            block["diag"] = work.tile([P, P], BF16, name="diag")
-            nc.vector.tensor_scalar_mul(block["diag"][:], ident_b[:], recip[:])
+        def make_diag(head):
+            recip = work.tile([P, TB], F32, name="recip")
+            nc.vector.reciprocal(recip[:], head["e_sum"][:])
+            head["diag"] = work.tile([P, TB, P], BF16, name="diag")
+            for tb in range(TB):
+                nc.vector.tensor_scalar_mul(head["diag"][:, tb, :], ident_b[:], recip[:, tb : tb + 1])
 
-        def turn(block, aT, tb):
-            aT_ps = psum.tile([P, TB, P], BF16, name="aT_ps", tag="bank")
-            for ub in range(TB):
-                for again in range(2):
-                    nc.tensor.matmul(
-                        aT_ps[:, ub, :], block["e"][:, ub * P : (ub + 1) * P], block["diag"][:],
-                        start=True, stop=True,
-                    )
-            if tb % 2 == 0:
-                nc.vector.tensor_copy(aT[:, :, tb * P : (tb + 1) * P], aT_ps[:])
-            else:
-                nc.scalar.copy(aT[:, :, tb * P : (tb + 1) * P], aT_ps[:])
+        def turn(head):
+            head["aT"] = work.tile([P, TB, T], BF16, name="aT")
+            for pair in range(TB // 2):
+                aT_ps = psum.tile([P, TB, 2 * P], BF16, name="aT_ps", tag="bank")
+                for half in range(2):
+                    tb = 2 * pair + half
+                    for ub in range(TB):
+                        nc.tensor.matmul(
+                            aT_ps[:, ub, half * P : (half + 1) * P],
+                            head["e"][:, tb, ub * P : (ub + 1) * P], head["diag"][:, tb, :],
+                            start=True, stop=True,
+                        )
+                nc.vector.tensor_copy(
+                    head["aT"][:, :, 2 * pair * P : 2 * (pair + 1) * P], aT_ps[:]
+                )
 
         av = {}
 
-        def weighted_sum(n, h, aT):
+        def weighted_sum(head, n, h):
             if h == 0:
                 av[n] = seq.tile([P, NH, T], BF16, name="av")
             av_ps = psum.tile([P, T], F32, name="av_ps", tag="bank")
             for ub in range(TB):
                 nc.tensor.matmul(
-                    av_ps[:], qkv[n]["v"][:, ub, h * P : (h + 1) * P], aT[:, ub, :],
+                    av_ps[:], qkv[n]["v"][:, ub, h * P : (h + 1) * P], head["aT"][:, ub, :],
                     start=ub == 0, stop=ub == TB - 1,
                 )
             nc.scalar.activation(av[n][:, h, :], av_ps[:], ACT.Identity, bias=column(1, h))
@@ -214,25 +217,28 @@ def tile_texttransformer_b_kernel(
                 nc.vector.scalar_tensor_tensor(
                     y[:, eb, :], y[:, eb, :], column(2, eb), mean_ps[:], ALU.add, ALU.subtract
                 )
-                nc.scalar.activation(norm[n]["sq"][:, eb, :], y[:, eb, :], ACT.Square)
 
-        def no_step():
-            pass
+        def square_step(n):
+            for eb in range(CB):
+                nc.scalar.activation(norm[n]["sq"][:, eb, :], x0[n][:, eb, :], ACT.Square)
 
         def var_step(n):
-            y = x0[n]
             var_ps = psum.tile([P, T], F32, name="var_ps", tag="bank")
             for eb in range(CB):
                 nc.tensor.matmul(
                     var_ps[:], mean_w[:], norm[n]["sq"][:, eb, :],
                     start=eb == 0, stop=eb == CB - 1,
                 )
-            log_var = seq.tile([P, T], F32, name="log_var")
-            nc.scalar.activation(log_var[:], var_ps[:], ACT.Ln, bias=eps_col[:])
-            rstd = seq.tile([P, T], F32, name="rstd")
-            nc.scalar.activation(rstd[:], log_var[:], ACT.Exp, scale=-0.5)
+            norm[n]["rstd"] = seq.tile([P, T], F32, name="rstd")
+            nc.scalar.activation(
+                norm[n]["rstd"][:], var_ps[:], ACT.Abs_reciprocal_sqrt, bias=eps_col[:]
+            )
+
+        def scale_step(n):
+            y = x0[n]
+            engine = nc.vector if n == B - 1 else nc.gpsimd
             for eb in range(CB):
-                nc.vector.tensor_tensor(y[:, eb, :], y[:, eb, :], rstd[:], ALU.mult)
+                engine.tensor_tensor(y[:, eb, :], y[:, eb, :], norm[n]["rstd"][:], ALU.mult)
                 nc.gpsimd.tensor_scalar(
                     y[:, eb, :], y[:, eb, :], column(3, eb), column(4, eb), ALU.mult, ALU.add
                 )
@@ -241,55 +247,63 @@ def tile_texttransformer_b_kernel(
         def finish_steps(n):
             return (
                 [(wo_step, (n, eb)) for eb in range(CB)]
-                + [(mean_step, (n,)), (no_step, ()), (var_step, (n,))]
+                + [(mean_step, (n,)), (square_step, (n,)), (var_step, (n,)), (scale_step, (n,))]
             )
 
-        def side_steps(n):
-            ahead = []
-            if n == 0:
-                ahead += [(project_group, (0, kind, g)) for kind, g in GROUPS[BANKS:]]
+        def project_steps(n):
+            steps = [(project_group, (n, kind, g)) for kind, g in GROUPS[BANKS:]]
             if n + 1 < B:
                 new_qkv(n + 1)
-                ahead += [(project_group, (n + 1, kind, g)) for kind, g in GROUPS]
-            behind = finish_steps(n - 1) if n > 0 else []
-            lead = (ahead + [(no_step, ())] * (SUM_LAG + 1))[: SUM_LAG + 1]
-            return lead + alternate(behind, ahead[SUM_LAG + 1 :])
+                steps += [(project_group, (n + 1, kind, g)) for kind, g in GROUPS[:BANKS]]
+            return steps
 
         new_qkv(0)
         first_ps = [psum.tile([P, T], F32, name=f"first_ps{i}", tag="bank") for i in range(BANKS)]
-        for c in range(CB):
-            for n in range(B if c < CB - 1 else 1):
+        for c in range(CB - 1):
+            for n in range(B):
                 look_up(c, n)
             for ps, (kind, g) in zip(first_ps, GROUPS):
                 project_matmul(ps, 0, kind, g, c)
-        for ps, (kind, g) in zip(first_ps, GROUPS):
+        look_up(CB - 1, 0)
+
+        def close_group(ps, kind, g):
+            project_matmul(ps, 0, kind, g, CB - 1)
             project_out(ps, 0, kind, g)
 
-        blocks = [(n, h, tb) for n in range(B) for h in range(NH) for tb in range(TB)]
-        soft = {}
-        aT = {}
-        for i in range(len(blocks) + SUM_LAG):
-            if i < len(blocks):
-                n, h, tb = blocks[i]
-                soft[i] = scores(n, h, tb)
-            if 0 <= i - DIAG_LAG < len(blocks):
-                make_diag(soft[i - DIAG_LAG])
-            if i < len(blocks):
+        open_groups = [(close_group, (ps, kind, g)) for ps, (kind, g) in zip(first_ps, GROUPS)]
+        for step, args in open_groups[:2]:
+            step(*args)
+
+        heads = {}
+        waiting = open_groups[2:]
+        taken = 0
+        for i in range((B * NH + 2) * TB):
+            k, tb = divmod(i, TB)
+            n, h = divmod(k, NH)
+            if n < B:
+                if tb == 0:
+                    heads[k] = new_head()
+                scores(heads[k], n, h, tb)
+            if tb == 0 and k - 1 in heads:
+                make_diag(heads[k - 1])
+            if n < B:
                 j = i % BLOCKS
                 if j == 0:
-                    steps = side_steps(n)
+                    ahead = project_steps(n)
                     if n + 1 < B:
                         look_up(CB - 1, n + 1)
-                for step, args in steps[len(steps) * j // BLOCKS : len(steps) * (j + 1) // BLOCKS]:
+                for step, args in ahead[len(GROUPS) * j // BLOCKS : len(GROUPS) * (j + 1) // BLOCKS]:
                     step(*args)
-            if 0 <= i - TURN_LAG < len(blocks):
-                n2, h2, tb2 = blocks[i - TURN_LAG]
-                if tb2 == 0:
-                    aT[n2, h2] = work.tile([P, TB, T], BF16, name="aT", bufs=2)
-                turn(soft[i - TURN_LAG], aT[n2, h2], tb2)
-            if 0 <= i - SUM_LAG:
-                n3, h3, tb3 = blocks[i - SUM_LAG]
-                if tb3 == TB - 1:
-                    weighted_sum(n3, h3, aT[n3, h3])
-        for step, args in finish_steps(B - 1):
+            if taken < len(waiting):
+                step, args = waiting[taken]
+                step(*args)
+                taken += 1
+            if tb == 1 and k - 2 in heads:
+                n2, h2 = divmod(k - 2, NH)
+                weighted_sum(heads[k - 2], n2, h2)
+                if h2 == NH - 1:
+                    waiting += finish_steps(n2)
+            if tb == TB - 1 and k - 1 in heads:
+                turn(heads[k - 1])
+        for step, args in waiting[taken:]:
             step(*args)

@@ -32,6 +32,15 @@ GROUPS = (
 
 BLOCKS = NH * TB
 
+PIECES = [(n, 0, TB) for n in range(B - 1)] + [(B - 1, 0, TB // 2), (B - 1, TB // 2, TB // 2)]
+
+
+def alternate(first, second):
+    merged = []
+    for i in range(max(len(first), len(second))):
+        merged += first[i : i + 1] + second[i : i + 1]
+    return merged
+
 
 def tile_texttransformer_b_kernel(
     tc, emb, pe, wq, bq, wk, wv, bv, wo, bo, gain, shift, offs, out
@@ -188,67 +197,86 @@ def tile_texttransformer_b_kernel(
 
         norm = {}
 
-        def wo_step(n, eb):
-            y = x0[n]
+        def y_of(p, eb):
+            n, first, blocks = PIECES[p]
+            return x0[n][:, eb, first * P : (first + blocks) * P]
+
+        def wo_step(p, eb):
+            n, first, blocks = PIECES[p]
+            width = blocks * P
             if eb == 0:
-                norm[n] = {name: seq.tile([P, CB, T], BF16, name=name) for name in ("yb", "sq")}
-            y_ps = psum.tile([P, T], F32, name="y_ps", tag="bank")
+                norm[p] = {
+                    name: seq.tile([P, CB, width], BF16, name=name) for name in ("yb", "sq")
+                }
+            y_ps = psum.tile([P, width], F32, name="y_ps", tag="bank")
             for h in range(NH):
                 nc.tensor.matmul(
-                    y_ps[:], weights["o"][:, h, eb * P : (eb + 1) * P], av[n][:, h, :],
+                    y_ps[:], weights["o"][:, h, eb * P : (eb + 1) * P],
+                    av[n][:, h, first * P : (first + blocks) * P],
                     start=h == 0, stop=h == NH - 1,
                 )
             nc.vector.scalar_tensor_tensor(
-                y[:, eb, :], y[:, eb, :], EMB_SCALE, y_ps[:], ALU.mult, ALU.add
+                y_of(p, eb), y_of(p, eb), EMB_SCALE, y_ps[:], ALU.mult, ALU.add
             )
             nc.gpsimd.tensor_scalar(
-                norm[n]["yb"][:, eb, :], y[:, eb, :], column(2, eb), 1.0, ALU.add, ALU.mult
+                norm[p]["yb"][:, eb, :], y_of(p, eb), column(2, eb), 1.0, ALU.add, ALU.mult
             )
 
-        def mean_step(n):
-            y = x0[n]
-            mean_ps = psum.tile([P, T], F32, name="mean_ps", tag="bank")
+        def mean_step(p):
+            mean_ps = psum.tile([P, PIECES[p][2] * P], F32, name="mean_ps", tag="bank")
             for eb in range(CB):
                 nc.tensor.matmul(
-                    mean_ps[:], mean_w[:], norm[n]["yb"][:, eb, :],
+                    mean_ps[:], mean_w[:], norm[p]["yb"][:, eb, :],
                     start=eb == 0, stop=eb == CB - 1,
                 )
             for eb in range(CB):
                 nc.vector.scalar_tensor_tensor(
-                    y[:, eb, :], y[:, eb, :], column(2, eb), mean_ps[:], ALU.add, ALU.subtract
+                    y_of(p, eb), y_of(p, eb), column(2, eb), mean_ps[:], ALU.add, ALU.subtract
                 )
 
-        def square_step(n):
+        def square_step(p):
             for eb in range(CB):
-                nc.scalar.activation(norm[n]["sq"][:, eb, :], x0[n][:, eb, :], ACT.Square)
+                nc.scalar.activation(norm[p]["sq"][:, eb, :], y_of(p, eb), ACT.Square)
 
-        def var_step(n):
-            var_ps = psum.tile([P, T], F32, name="var_ps", tag="bank")
+        def var_step(p):
+            width = PIECES[p][2] * P
+            var_ps = psum.tile([P, width], F32, name="var_ps", tag="bank")
             for eb in range(CB):
                 nc.tensor.matmul(
-                    var_ps[:], mean_w[:], norm[n]["sq"][:, eb, :],
+                    var_ps[:], mean_w[:], norm[p]["sq"][:, eb, :],
                     start=eb == 0, stop=eb == CB - 1,
                 )
-            norm[n]["rstd"] = seq.tile([P, T], F32, name="rstd")
+            norm[p]["rstd"] = seq.tile([P, width], F32, name="rstd")
             nc.scalar.activation(
-                norm[n]["rstd"][:], var_ps[:], ACT.Abs_reciprocal_sqrt, bias=eps_col[:]
+                norm[p]["rstd"][:], var_ps[:], ACT.Abs_reciprocal_sqrt, bias=eps_col[:]
             )
 
-        def scale_step(n):
-            y = x0[n]
+        def scale_step(p):
+            n, first, blocks = PIECES[p]
             engine = nc.vector if n == B - 1 else nc.gpsimd
             for eb in range(CB):
-                engine.tensor_tensor(y[:, eb, :], y[:, eb, :], norm[n]["rstd"][:], ALU.mult)
+                engine.tensor_tensor(y_of(p, eb), y_of(p, eb), norm[p]["rstd"][:], ALU.mult)
                 nc.gpsimd.tensor_scalar(
-                    y[:, eb, :], y[:, eb, :], column(3, eb), column(4, eb), ALU.mult, ALU.add
+                    y_of(p, eb), y_of(p, eb), column(3, eb), column(4, eb), ALU.mult, ALU.add
                 )
-                nc.sync.dma_start(out[eb * P : (eb + 1) * P, n * T : (n + 1) * T], y[:, eb, :])
+                nc.sync.dma_start(
+                    out[eb * P : (eb + 1) * P, n * T + first * P : n * T + (first + blocks) * P],
+                    y_of(p, eb),
+                )
+
+        def piece_steps(p):
+            return (
+                [(wo_step, (p, eb)) for eb in range(CB)]
+                + [(mean_step, (p,)), (square_step, (p,)), (var_step, (p,)), (scale_step, (p,))]
+            )
 
         def finish_steps(n):
-            return (
-                [(wo_step, (n, eb)) for eb in range(CB)]
-                + [(mean_step, (n,)), (square_step, (n,)), (var_step, (n,)), (scale_step, (n,))]
-            )
+            steps = []
+            for p in range(len(PIECES)):
+                if PIECES[p][0] == n:
+                    later = piece_steps(p)
+                    steps = steps[:CB] + alternate(later[:CB], steps[CB:]) + later[CB:]
+            return steps
 
         def project_steps(n):
             steps = [(project_group, (n, kind, g)) for kind, g in GROUPS[BANKS:]]

@@ -159,12 +159,13 @@ def tile_texttransformer_b_kernel(
                 accum_out=head["e_sum"][:, tb : tb + 1],
             )
 
-        def make_diag(head):
+        def normalize(head):
             recip = work.tile([P, TB], F32, name="recip")
             nc.vector.reciprocal(recip[:], head["e_sum"][:])
-            head["diag"] = work.tile([P, TB, P], BF16, name="diag")
             for tb in range(TB):
-                nc.vector.tensor_scalar_mul(head["diag"][:, tb, :], ident_b[:], recip[:, tb : tb + 1])
+                nc.vector.tensor_scalar_mul(
+                    head["e"][:, tb, :], head["e"][:, tb, :], recip[:, tb : tb + 1]
+                )
 
         def turn(head):
             head["aT"] = work.tile([P, TB, T], BF16, name="aT")
@@ -173,10 +174,9 @@ def tile_texttransformer_b_kernel(
                 for half in range(2):
                     tb = 2 * pair + half
                     for ub in range(TB):
-                        nc.tensor.matmul(
+                        nc.tensor.transpose(
                             aT_ps[:, ub, half * P : (half + 1) * P],
-                            head["e"][:, tb, ub * P : (ub + 1) * P], head["diag"][:, tb, :],
-                            start=True, stop=True,
+                            head["e"][:, tb, ub * P : (ub + 1) * P], ident_b[:],
                         )
                 nc.vector.tensor_copy(
                     head["aT"][:, :, 2 * pair * P : 2 * (pair + 1) * P], aT_ps[:]
@@ -313,7 +313,7 @@ def tile_texttransformer_b_kernel(
                     heads[k] = new_head()
                 scores(heads[k], n, h, tb)
             if tb == 0 and k - 1 in heads:
-                make_diag(heads[k - 1])
+                normalize(heads[k - 1])
             if n < B:
                 j = i % BLOCKS
                 if j == 0:

@@ -107,9 +107,7 @@ def tile_texttransformer_b_kernel(
             nc.vector.tensor_tensor(
                 x0[n][:, c, :], table[c][:].indirect(piece), pe_sb[:, c, :], ALU.add
             )
-            nc.gpsimd.tensor_scalar(
-                x0b[n][:, c, :], x0[n][:, c, :], EMB_SCALE, 0.0, ALU.mult, ALU.add
-            )
+            nc.scalar.mul(x0b[n][:, c, :], x0[n][:, c, :], EMB_SCALE)
 
         qkv = {}
 

@@ -216,9 +216,7 @@ def tile_texttransformer_b_kernel(
             nc.vector.scalar_tensor_tensor(
                 y_of(p, eb), y_of(p, eb), EMB_SCALE, y_ps[:], ALU.mult, ALU.add
             )
-            nc.gpsimd.tensor_scalar(
-                norm[p]["yb"][:, eb, :], y_of(p, eb), column(2, eb), 1.0, ALU.add, ALU.mult
-            )
+            nc.scalar.activation(norm[p]["yb"][:, eb, :], y_of(p, eb), ACT.Identity, bias=column(2, eb))
 
         def mean_step(p):
             mean_ps = psum.tile([P, PIECES[p][2] * P], F32, name="mean_ps", tag="bank")
@@ -251,11 +249,10 @@ def tile_texttransformer_b_kernel(
 
         def scale_step(p):
             n, first, blocks = PIECES[p]
-            engine = nc.vector if n == B - 1 else nc.gpsimd
             for eb in range(CB):
-                engine.tensor_tensor(y_of(p, eb), y_of(p, eb), norm[p]["rstd"][:], ALU.mult)
-                nc.gpsimd.tensor_scalar(
-                    y_of(p, eb), y_of(p, eb), column(3, eb), column(4, eb), ALU.mult, ALU.add
+                nc.vector.tensor_tensor(y_of(p, eb), y_of(p, eb), norm[p]["rstd"][:], ALU.mult)
+                nc.scalar.activation(
+                    y_of(p, eb), y_of(p, eb), ACT.Identity, bias=column(4, eb), scale=column(3, eb)
                 )
                 nc.sync.dma_start(
                     out[eb * P : (eb + 1) * P, n * T + first * P : n * T + (first + blocks) * P],

@@ -24,11 +24,7 @@ EMB_SCALE = math.sqrt(D)
 
 FLOPS = 2 * D * D * B * T * 4 + 2 * 2 * B * NH * T * T * P
 
-GROUPS = (
-    [(kind, g) for g in (0, 1) for kind in ("q", "k")]
-    + [("v", g) for g in range(TB)]
-    + [(kind, g) for g in (2, 3) for kind in ("q", "k")]
-)
+GROUPS = [(kind, g) for g in range(NH) for kind in ("q", "k")] + [("v", g) for g in range(TB)]
 
 BLOCKS = NH * TB
 
@@ -79,7 +75,7 @@ def tile_texttransformer_b_kernel(
             if c == 0:
                 load_weights("q", wq)
                 load_weights("k", wk)
-                load_weights("v", wv)
+        load_weights("v", wv)
         load_weights("o", wo)
 
         ident_f = held.tile([P, P], F32, name="ident_f")
@@ -98,6 +94,25 @@ def tile_texttransformer_b_kernel(
         nc.vector.memset(mean_w[:], 1.0 / D)
         eps_col = held.tile([P, 1], F32, name="eps_col")
         nc.vector.memset(eps_col[:], EPS)
+
+        bo_b = held.tile([P, CB], BF16, name="bo_b")
+        nc.vector.tensor_copy(bo_b[:], vec_cols[:, 2 * CB : 3 * CB])
+        bo_ps = psum.tile([P, CB], F32, name="bo_ps", tag="bank")
+        nc.tensor.matmul(bo_ps[:], mean_w[:], bo_b[:], start=True, stop=True)
+        bo_mean = held.tile([P, 1], F32, name="bo_mean")
+        nc.vector.reduce_sum(bo_mean[:], bo_ps[:], axis=AX.X)
+        bo_centred = held.tile([P, CB], F32, name="bo_centred")
+        nc.vector.tensor_scalar_sub(bo_centred[:], vec_cols[:, 2 * CB : 3 * CB], bo_mean[:])
+
+        def center_wo():
+            row_mean = held.tile([P, CB], F32, name="row_mean")
+            for c in range(CB):
+                nc.vector.reduce_sum(row_mean[:, c : c + 1], weights["o"][:, c, :], axis=AX.X)
+            nc.vector.tensor_scalar_mul(row_mean[:], row_mean[:], 1.0 / D)
+            for c in range(CB):
+                nc.vector.tensor_scalar_sub(
+                    weights["o"][:, c, :], weights["o"][:, c, :], row_mean[:, c : c + 1]
+                )
 
         x0 = [held.tile([P, CB, T], F32, name=f"x0_{n}") for n in range(B)]
         x0b = [held.tile([P, CB, T], BF16, name=f"x0b_{n}") for n in range(B)]
@@ -195,6 +210,17 @@ def tile_texttransformer_b_kernel(
 
         norm = {}
 
+        def center_x0(n):
+            mean_ps = psum.tile([P, T], F32, name="mean_ps", tag="bank")
+            for c in range(CB):
+                nc.tensor.matmul(
+                    mean_ps[:], mean_w[:], x0b[n][:, c, :], start=c == 0, stop=c == CB - 1
+                )
+            for c in range(CB):
+                nc.vector.scalar_tensor_tensor(
+                    x0[n][:, c, :], x0[n][:, c, :], EMB_SCALE, mean_ps[:], ALU.mult, ALU.subtract
+                )
+
         def y_of(p, eb):
             n, first, blocks = PIECES[p]
             return x0[n][:, eb, first * P : (first + blocks) * P]
@@ -203,9 +229,7 @@ def tile_texttransformer_b_kernel(
             n, first, blocks = PIECES[p]
             width = blocks * P
             if eb == 0:
-                norm[p] = {
-                    name: seq.tile([P, CB, width], BF16, name=name) for name in ("yb", "sq")
-                }
+                norm[p] = {"sq": seq.tile([P, CB, width], BF16, name="sq")}
             y_ps = psum.tile([P, width], F32, name="y_ps", tag="bank")
             for h in range(NH):
                 nc.tensor.matmul(
@@ -214,25 +238,9 @@ def tile_texttransformer_b_kernel(
                     start=h == 0, stop=h == NH - 1,
                 )
             nc.vector.scalar_tensor_tensor(
-                y_of(p, eb), y_of(p, eb), EMB_SCALE, y_ps[:], ALU.mult, ALU.add
+                y_of(p, eb), y_of(p, eb), bo_centred[:, eb : eb + 1], y_ps[:], ALU.add, ALU.add
             )
-            nc.scalar.activation(norm[p]["yb"][:, eb, :], y_of(p, eb), ACT.Identity, bias=column(2, eb))
-
-        def mean_step(p):
-            mean_ps = psum.tile([P, PIECES[p][2] * P], F32, name="mean_ps", tag="bank")
-            for eb in range(CB):
-                nc.tensor.matmul(
-                    mean_ps[:], mean_w[:], norm[p]["yb"][:, eb, :],
-                    start=eb == 0, stop=eb == CB - 1,
-                )
-            for eb in range(CB):
-                nc.vector.scalar_tensor_tensor(
-                    y_of(p, eb), y_of(p, eb), column(2, eb), mean_ps[:], ALU.add, ALU.subtract
-                )
-
-        def square_step(p):
-            for eb in range(CB):
-                nc.scalar.activation(norm[p]["sq"][:, eb, :], y_of(p, eb), ACT.Square)
+            nc.scalar.activation(norm[p]["sq"][:, eb, :], y_of(p, eb), ACT.Square)
 
         def var_step(p):
             width = PIECES[p][2] * P
@@ -262,7 +270,7 @@ def tile_texttransformer_b_kernel(
         def piece_steps(p):
             return (
                 [(wo_step, (p, eb)) for eb in range(CB)]
-                + [(mean_step, (p,)), (square_step, (p,)), (var_step, (p,)), (scale_step, (p,))]
+                + [(var_step, (p,)), (scale_step, (p,))]
             )
 
         def finish_steps(n):
@@ -315,6 +323,9 @@ def tile_texttransformer_b_kernel(
                     ahead = project_steps(n)
                     if n + 1 < B:
                         look_up(CB - 1, n + 1)
+                    if n == 0:
+                        waiting.append((center_wo, ()))
+                    waiting.append((center_x0, (n,)))
                 for step, args in ahead[len(GROUPS) * j // BLOCKS : len(GROUPS) * (j + 1) // BLOCKS]:
                     step(*args)
             if taken < len(waiting):
@@ -324,8 +335,10 @@ def tile_texttransformer_b_kernel(
             if tb == 1 and k - 2 in heads:
                 n2, h2 = divmod(k - 2, NH)
                 weighted_sum(heads[k - 2], n2, h2)
-                if h2 == NH - 1:
+                if h2 == NH - 1 and n2 != B - 2:
                     waiting += finish_steps(n2)
+            if (k, tb) == (B * NH - 1, 0):
+                waiting += finish_steps(B - 2)
             if tb == TB - 1 and k - 1 in heads:
                 turn(heads[k - 1])
         for step, args in waiting[taken:]:

@@ -27,15 +27,9 @@ FLOPS = 2 * D * D * B * T * 4 + 2 * 2 * B * NH * T * T * P
 GROUPS = [(kind, g) for g in range(NH) for kind in ("q", "k")] + [("v", g) for g in range(TB)]
 
 BLOCKS = NH * TB
+DRAIN = 20
 
 PIECES = [(n, 0, TB) for n in range(B - 1)] + [(B - 1, 0, TB // 2), (B - 1, TB // 2, TB // 2)]
-
-
-def alternate(first, second):
-    merged = []
-    for i in range(max(len(first), len(second))):
-        merged += first[i : i + 1] + second[i : i + 1]
-    return merged
 
 
 def tile_texttransformer_b_kernel(
@@ -124,6 +118,11 @@ def tile_texttransformer_b_kernel(
             )
             nc.scalar.mul(x0b[n][:, c, :], x0[n][:, c, :], EMB_SCALE)
 
+        due_next = []
+
+        def in_next_block(step, *args):
+            due_next.append((step, args))
+
         qkv = {}
 
         def new_qkv(n):
@@ -150,7 +149,7 @@ def tile_texttransformer_b_kernel(
             ps = psum.tile([P, T], F32, name="proj_ps", tag="bank")
             for c in range(CB):
                 project_matmul(ps, n, kind, g, c)
-            project_out(ps, n, kind, g)
+            in_next_block(project_out, ps, n, kind, g)
 
         def new_head():
             return {
@@ -159,12 +158,15 @@ def tile_texttransformer_b_kernel(
                 "e_sum": work.tile([P, TB], F32, name="e_sum"),
             }
 
-        def scores(head, n, h, tb):
+        def scores(n, h, tb):
             s_ps = psum.tile([P, T], F32, name="s_ps", tag="bank")
             nc.tensor.matmul(
                 s_ps[:], qkv[n]["q"][:, h, tb * P : (tb + 1) * P], qkv[n]["k"][:, h, :],
                 start=True, stop=True,
             )
+            return s_ps
+
+        def exponentials(head, s_ps, tb):
             neg_max = head["neg_max"][:, tb : tb + 1]
             nc.vector.reduce_max(neg_max, s_ps[:], axis=AX.X, negate=True)
             nc.scalar.activation(
@@ -191,8 +193,8 @@ def tile_texttransformer_b_kernel(
                             aT_ps[:, ub, half * P : (half + 1) * P],
                             head["e"][:, tb, ub * P : (ub + 1) * P], ident_b[:],
                         )
-                nc.vector.tensor_copy(
-                    head["aT"][:, :, 2 * pair * P : 2 * (pair + 1) * P], aT_ps[:]
+                in_next_block(
+                    nc.vector.tensor_copy, head["aT"][:, :, 2 * pair * P : 2 * (pair + 1) * P], aT_ps[:]
                 )
 
         av = {}
@@ -206,16 +208,28 @@ def tile_texttransformer_b_kernel(
                     av_ps[:], qkv[n]["v"][:, ub, h * P : (h + 1) * P], head["aT"][:, ub, :],
                     start=ub == 0, stop=ub == TB - 1,
                 )
+            in_next_block(av_out, av_ps, n, h)
+
+        def av_out(av_ps, n, h):
             nc.scalar.activation(av[n][:, h, :], av_ps[:], ACT.Identity, bias=column(1, h))
 
         norm = {}
 
         def center_x0(n):
+            two_blocks = work.tile([P, CB // 2, T], BF16, name="two_blocks")
+            nc.gpsimd.tensor_tensor(
+                two_blocks[:], x0b[n][:, 0 : CB // 2, :], x0b[n][:, CB // 2 : CB, :], ALU.add
+            )
+            one_block = work.tile([P, T], BF16, name="one_block")
+            nc.gpsimd.tensor_tensor(one_block[:], two_blocks[:, 0, :], two_blocks[:, 1, :], ALU.add)
+            in_next_block(in_next_block, center_matmul, n, one_block)
+
+        def center_matmul(n, one_block):
             mean_ps = psum.tile([P, T], F32, name="mean_ps", tag="bank")
-            for c in range(CB):
-                nc.tensor.matmul(
-                    mean_ps[:], mean_w[:], x0b[n][:, c, :], start=c == 0, stop=c == CB - 1
-                )
+            nc.tensor.matmul(mean_ps[:], mean_w[:], one_block[:], start=True, stop=True)
+            in_next_block(center_subtract, n, mean_ps)
+
+        def center_subtract(n, mean_ps):
             for c in range(CB):
                 nc.vector.scalar_tensor_tensor(
                     x0[n][:, c, :], x0[n][:, c, :], EMB_SCALE, mean_ps[:], ALU.mult, ALU.subtract
@@ -237,28 +251,44 @@ def tile_texttransformer_b_kernel(
                     av[n][:, h, first * P : (first + blocks) * P],
                     start=h == 0, stop=h == NH - 1,
                 )
+            in_next_block(residual, p, eb, y_ps)
+
+        def residual(p, eb, y_ps):
             nc.vector.scalar_tensor_tensor(
                 y_of(p, eb), y_of(p, eb), bo_centred[:, eb : eb + 1], y_ps[:], ALU.add, ALU.add
             )
-            nc.scalar.activation(norm[p]["sq"][:, eb, :], y_of(p, eb), ACT.Square)
+            in_next_block(square, p, eb)
 
-        def var_step(p):
-            width = PIECES[p][2] * P
-            var_ps = psum.tile([P, width], F32, name="var_ps", tag="bank")
-            for eb in range(CB):
-                nc.tensor.matmul(
-                    var_ps[:], mean_w[:], norm[p]["sq"][:, eb, :],
-                    start=eb == 0, stop=eb == CB - 1,
-                )
-            norm[p]["rstd"] = seq.tile([P, width], F32, name="rstd")
-            nc.scalar.activation(
-                norm[p]["rstd"][:], var_ps[:], ACT.Abs_reciprocal_sqrt, bias=eps_col[:]
+        def square(p, eb):
+            nc.scalar.activation(norm[p]["sq"][:, eb, :], y_of(p, eb), ACT.Square)
+            in_next_block(var_matmul, p, eb)
+
+        def var_matmul(p, eb):
+            if eb == 0:
+                norm[p]["var_ps"] = psum.tile([P, PIECES[p][2] * P], F32, name="var_ps", tag="bank")
+            nc.tensor.matmul(
+                norm[p]["var_ps"][:], mean_w[:], norm[p]["sq"][:, eb, :],
+                start=eb == 0, stop=eb == CB - 1,
             )
+            if eb == CB - 1:
+                in_next_block(rstd_step, p)
+
+        def rstd_step(p):
+            norm[p]["rstd"] = seq.tile([P, PIECES[p][2] * P], F32, name="rstd")
+            nc.scalar.activation(
+                norm[p]["rstd"][:], norm[p]["var_ps"][:], ACT.Abs_reciprocal_sqrt, bias=eps_col[:]
+            )
+            in_next_block(scale_step, p)
 
         def scale_step(p):
             n, first, blocks = PIECES[p]
             for eb in range(CB):
                 nc.vector.tensor_tensor(y_of(p, eb), y_of(p, eb), norm[p]["rstd"][:], ALU.mult)
+            in_next_block(affine_step, p)
+
+        def affine_step(p):
+            n, first, blocks = PIECES[p]
+            for eb in range(CB):
                 nc.scalar.activation(
                     y_of(p, eb), y_of(p, eb), ACT.Identity, bias=column(4, eb), scale=column(3, eb)
                 )
@@ -267,19 +297,10 @@ def tile_texttransformer_b_kernel(
                     y_of(p, eb),
                 )
 
-        def piece_steps(p):
-            return (
-                [(wo_step, (p, eb)) for eb in range(CB)]
-                + [(var_step, (p,)), (scale_step, (p,))]
-            )
-
         def finish_steps(n):
-            steps = []
-            for p in range(len(PIECES)):
-                if PIECES[p][0] == n:
-                    later = piece_steps(p)
-                    steps = steps[:CB] + alternate(later[:CB], steps[CB:]) + later[CB:]
-            return steps
+            return [
+                (wo_step, (p, eb)) for p in range(len(PIECES)) if PIECES[p][0] == n for eb in range(CB)
+            ]
 
         def project_steps(n):
             steps = [(project_group, (n, kind, g)) for kind, g in GROUPS[BANKS:]]
@@ -301,20 +322,29 @@ def tile_texttransformer_b_kernel(
             project_matmul(ps, 0, kind, g, CB - 1)
             project_out(ps, 0, kind, g)
 
-        open_groups = [(close_group, (ps, kind, g)) for ps, (kind, g) in zip(first_ps, GROUPS)]
+        def close_group_later(ps, kind, g):
+            project_matmul(ps, 0, kind, g, CB - 1)
+            in_next_block(project_out, ps, 0, kind, g)
+
+        open_groups = [(close_group_later, (ps, kind, g)) for ps, (kind, g) in zip(first_ps, GROUPS)]
         for step, args in open_groups[:2]:
-            step(*args)
+            close_group(*args)
 
         heads = {}
         waiting = open_groups[2:]
-        taken = 0
-        for i in range((B * NH + 2) * TB):
+        for i in range((B * NH + 2) * TB + DRAIN):
             k, tb = divmod(i, TB)
             n, h = divmod(k, NH)
             if n < B:
                 if tb == 0:
                     heads[k] = new_head()
-                scores(heads[k], n, h, tb)
+                s_ps = scores(n, h, tb)
+            due = list(due_next)
+            due_next.clear()
+            for step, args in due:
+                step(*args)
+            if n < B:
+                exponentials(heads[k], s_ps, tb)
             if tb == 0 and k - 1 in heads:
                 normalize(heads[k - 1])
             if n < B:
@@ -328,18 +358,16 @@ def tile_texttransformer_b_kernel(
                     waiting.append((center_x0, (n,)))
                 for step, args in ahead[len(GROUPS) * j // BLOCKS : len(GROUPS) * (j + 1) // BLOCKS]:
                     step(*args)
-            if taken < len(waiting):
-                step, args = waiting[taken]
+            if waiting:
+                step, args = waiting.pop(0)
                 step(*args)
-                taken += 1
             if tb == 1 and k - 2 in heads:
                 n2, h2 = divmod(k - 2, NH)
                 weighted_sum(heads[k - 2], n2, h2)
                 if h2 == NH - 1 and n2 != B - 2:
-                    waiting += finish_steps(n2)
+                    in_next_block(waiting.extend, finish_steps(n2))
             if (k, tb) == (B * NH - 1, 0):
                 waiting += finish_steps(B - 2)
             if tb == TB - 1 and k - 1 in heads:
                 turn(heads[k - 1])
-        for step, args in waiting[taken:]:
-            step(*args)
+        assert not waiting and not due_next

@@ -217,12 +217,12 @@ def tile_texttransformer_b_kernel(
 
         def center_x0(n):
             two_blocks = work.tile([P, CB // 2, T], BF16, name="two_blocks")
-            nc.gpsimd.tensor_tensor(
+            nc.vector.tensor_tensor(
                 two_blocks[:], x0b[n][:, 0 : CB // 2, :], x0b[n][:, CB // 2 : CB, :], ALU.add
             )
             one_block = work.tile([P, T], BF16, name="one_block")
-            nc.gpsimd.tensor_tensor(one_block[:], two_blocks[:, 0, :], two_blocks[:, 1, :], ALU.add)
-            in_next_block(in_next_block, center_matmul, n, one_block)
+            nc.vector.tensor_tensor(one_block[:], two_blocks[:, 0, :], two_blocks[:, 1, :], ALU.add)
+            in_next_block(center_matmul, n, one_block)
 
         def center_matmul(n, one_block):
             mean_ps = psum.tile([P, T], F32, name="mean_ps", tag="bank")

@@ -27,6 +27,11 @@ FLOPS = 2 * D * D * B * T * 4 + 2 * 2 * B * NH * T * T * P
 GROUPS = [(kind, g) for g in range(NH) for kind in ("q", "k")] + [("v", g) for g in range(TB)]
 
 BLOCKS = NH * TB
+HALVES = 2
+HB = TB // HALVES
+HT = HB * P
+
+PARTS = [(n, half, h) for n in range(B) for half in range(HALVES) for h in range(NH)]
 DRAIN = 20
 
 PIECES = [(n, 0, TB) for n in range(B - 1)] + [(B - 1, 0, TB // 2), (B - 1, TB // 2, TB // 2)]
@@ -39,7 +44,7 @@ def tile_texttransformer_b_kernel(
     with (
         tc.tile_pool(name="held", bufs=1) as held,
         tc.tile_pool(name="seq", bufs=2) as seq,
-        tc.tile_pool(name="work", bufs=3) as work,
+        tc.tile_pool(name="work", bufs=4) as work,
         tc.psum_pool(name="psum", bufs=BANKS) as psum,
     ):
         offsets = held.tile([P, B * T // 16], U16, name="offsets")
@@ -83,6 +88,9 @@ def tile_texttransformer_b_kernel(
 
         def column(v, b):
             return vec_cols[:, v * CB + b : v * CB + b + 1]
+
+        bq_scaled = held.tile([P, NH], F32, name="bq_scaled")
+        nc.vector.tensor_scalar_mul(bq_scaled[:], vec_cols[:, 0:NH], 1.0 / math.sqrt(P))
 
         mean_w = held.tile([P, P], BF16, name="mean_w")
         nc.vector.memset(mean_w[:], 1.0 / D)
@@ -139,8 +147,8 @@ def tile_texttransformer_b_kernel(
         def project_out(ps, n, kind, g):
             dest = qkv[n][kind][:, g, :]
             if kind == "q":
-                nc.vector.tensor_scalar(
-                    dest, ps[:], column(0, g), 1.0 / math.sqrt(P), ALU.add, ALU.mult
+                nc.scalar.activation(
+                    dest, ps[:], ACT.Identity, bias=bq_scaled[:, g : g + 1], scale=1.0 / math.sqrt(P)
                 )
             else:
                 nc.scalar.copy(dest, ps[:])
@@ -151,78 +159,80 @@ def tile_texttransformer_b_kernel(
                 project_matmul(ps, n, kind, g, c)
             in_next_block(project_out, ps, n, kind, g)
 
-        def new_head():
+        def new_part():
             return {
-                "neg_max": work.tile([P, TB], F32, name="neg_max"),
-                "e": work.tile([P, TB, T], BF16, name="e"),
-                "e_sum": work.tile([P, TB], F32, name="e_sum"),
+                "neg_max": work.tile([P, HB], F32, name="neg_max"),
+                "e": work.tile([P, HB, T], BF16, name="e"),
+                "e_sum": work.tile([P, HB], F32, name="e_sum"),
             }
 
-        def scores(n, h, tb):
+        def scores(n, half, h, b):
+            first = half * HT + b * P
             s_ps = psum.tile([P, T], F32, name="s_ps", tag="bank")
             nc.tensor.matmul(
-                s_ps[:], qkv[n]["q"][:, h, tb * P : (tb + 1) * P], qkv[n]["k"][:, h, :],
+                s_ps[:], qkv[n]["q"][:, h, first : first + P], qkv[n]["k"][:, h, :],
                 start=True, stop=True,
             )
             return s_ps
 
-        def exponentials(head, s_ps, tb):
-            neg_max = head["neg_max"][:, tb : tb + 1]
+        def exponentials(part, s_ps, tb):
+            neg_max = part["neg_max"][:, tb : tb + 1]
             nc.vector.reduce_max(neg_max, s_ps[:], axis=AX.X, negate=True)
             nc.scalar.activation(
-                head["e"][:, tb, :], s_ps[:], ACT.Exp, bias=neg_max, scale=1.0,
-                accum_out=head["e_sum"][:, tb : tb + 1],
+                part["e"][:, tb, :], s_ps[:], ACT.Exp, bias=neg_max, scale=1.0,
+                accum_out=part["e_sum"][:, tb : tb + 1],
             )
 
-        def normalize(head):
-            recip = work.tile([P, TB], F32, name="recip")
-            nc.vector.reciprocal(recip[:], head["e_sum"][:])
-            for tb in range(TB):
+        def normalize(part):
+            recip = work.tile([P, HB], F32, name="recip")
+            nc.vector.reciprocal(recip[:], part["e_sum"][:])
+            for tb in range(HB):
                 nc.vector.tensor_scalar_mul(
-                    head["e"][:, tb, :], head["e"][:, tb, :], recip[:, tb : tb + 1]
+                    part["e"][:, tb, :], part["e"][:, tb, :], recip[:, tb : tb + 1]
                 )
 
-        def turn(head):
-            head["aT"] = work.tile([P, TB, T], BF16, name="aT")
-            for pair in range(TB // 2):
-                aT_ps = psum.tile([P, TB, 2 * P], BF16, name="aT_ps", tag="bank")
-                for half in range(2):
-                    tb = 2 * pair + half
-                    for ub in range(TB):
-                        nc.tensor.transpose(
-                            aT_ps[:, ub, half * P : (half + 1) * P],
-                            head["e"][:, tb, ub * P : (ub + 1) * P], ident_b[:],
-                        )
-                in_next_block(
-                    nc.vector.tensor_copy, head["aT"][:, :, 2 * pair * P : 2 * (pair + 1) * P], aT_ps[:]
-                )
+        def turn(part):
+            part["aT"] = work.tile([P, TB, HT], BF16, name="aT")
+            aT_ps = psum.tile([P, TB, HT], BF16, name="aT_ps", tag="bank")
+            for tb in range(HB):
+                for ub in range(TB):
+                    nc.tensor.transpose(
+                        aT_ps[:, ub, tb * P : (tb + 1) * P],
+                        part["e"][:, tb, ub * P : (ub + 1) * P], ident_b[:],
+                    )
+            in_next_block(nc.vector.tensor_copy, part["aT"][:], aT_ps[:])
 
         av = {}
 
-        def weighted_sum(head, n, h):
-            if h == 0:
+        def weighted_sum(part, n, half, h):
+            if half == 0 and h == 0:
                 av[n] = seq.tile([P, NH, T], BF16, name="av")
-            av_ps = psum.tile([P, T], F32, name="av_ps", tag="bank")
+            av_ps = psum.tile([P, HT], F32, name="av_ps", tag="bank")
             for ub in range(TB):
                 nc.tensor.matmul(
-                    av_ps[:], qkv[n]["v"][:, ub, h * P : (h + 1) * P], head["aT"][:, ub, :],
+                    av_ps[:], qkv[n]["v"][:, ub, h * P : (h + 1) * P], part["aT"][:, ub, :],
                     start=ub == 0, stop=ub == TB - 1,
                 )
-            in_next_block(av_out, av_ps, n, h)
+            in_next_block(av_out, av_ps, n, half, h)
 
-        def av_out(av_ps, n, h):
-            nc.scalar.activation(av[n][:, h, :], av_ps[:], ACT.Identity, bias=column(1, h))
+        def av_out(av_ps, n, half, h):
+            nc.scalar.activation(
+                av[n][:, h, half * HT : (half + 1) * HT], av_ps[:], ACT.Identity, bias=column(1, h)
+            )
 
         norm = {}
 
-        def center_x0(n):
+        def sum_of_blocks(blocks):
             two_blocks = work.tile([P, CB // 2, T], BF16, name="two_blocks")
             nc.vector.tensor_tensor(
-                two_blocks[:], x0b[n][:, 0 : CB // 2, :], x0b[n][:, CB // 2 : CB, :], ALU.add
+                two_blocks[:], blocks[:, 0 : CB // 2, :], blocks[:, CB // 2 : CB, :], ALU.add
             )
             one_block = work.tile([P, T], BF16, name="one_block")
             nc.vector.tensor_tensor(one_block[:], two_blocks[:, 0, :], two_blocks[:, 1, :], ALU.add)
-            in_next_block(center_matmul, n, one_block)
+            return one_block
+
+        def center_x0(n):
+            in_next_block(center_matmul, n, sum_of_blocks(x0b[n]))
 
         def center_matmul(n, one_block):
             mean_ps = psum.tile([P, T], F32, name="mean_ps", tag="bank")
@@ -261,7 +271,18 @@ def tile_texttransformer_b_kernel(
 
         def square(p, eb):
             nc.scalar.activation(norm[p]["sq"][:, eb, :], y_of(p, eb), ACT.Square)
-            in_next_block(var_matmul, p, eb)
+            if PIECES[p][0] >= B - 2:
+                in_next_block(var_matmul, p, eb)
+            elif eb == CB - 1:
+                in_next_block(sum_of_squares, p)
+
+        def sum_of_squares(p):
+            in_next_block(var_of_sum, p, sum_of_blocks(norm[p]["sq"]))
+
+        def var_of_sum(p, one_block):
+            norm[p]["var_ps"] = psum.tile([P, T], F32, name="var_ps", tag="bank")
+            nc.tensor.matmul(norm[p]["var_ps"][:], mean_w[:], one_block[:], start=True, stop=True)
+            in_next_block(rstd_step, p)
 
         def var_matmul(p, eb):
             if eb == 0:
@@ -297,9 +318,12 @@ def tile_texttransformer_b_kernel(
                     y_of(p, eb),
                 )
 
-        def finish_steps(n):
+        def finish_steps(n, blocks_done):
             return [
-                (wo_step, (p, eb)) for p in range(len(PIECES)) if PIECES[p][0] == n for eb in range(CB)
+                (wo_step, (p, eb))
+                for p in range(len(PIECES))
+                if (n, blocks_done) == (PIECES[p][0], PIECES[p][1] + PIECES[p][2])
+                for eb in range(CB)
             ]
 
         def project_steps(n):
@@ -327,27 +351,27 @@ def tile_texttransformer_b_kernel(
             in_next_block(project_out, ps, 0, kind, g)
 
         open_groups = [(close_group_later, (ps, kind, g)) for ps, (kind, g) in zip(first_ps, GROUPS)]
-        for step, args in open_groups[:2]:
+        for step, args in open_groups[:4]:
             close_group(*args)
 
-        heads = {}
-        waiting = open_groups[2:]
-        for i in range((B * NH + 2) * TB + DRAIN):
-            k, tb = divmod(i, TB)
-            n, h = divmod(k, NH)
-            if n < B:
-                if tb == 0:
-                    heads[k] = new_head()
-                s_ps = scores(n, h, tb)
+        parts = {}
+        waiting = open_groups[4:]
+        for i in range((len(PARTS) + 3) * HB + DRAIN):
+            k, b = divmod(i, HB)
+            if k < len(PARTS):
+                n, half, h = PARTS[k]
+                if b == 0:
+                    parts[k] = new_part()
+                s_ps = scores(n, half, h, b)
             due = list(due_next)
             due_next.clear()
             for step, args in due:
                 step(*args)
-            if n < B:
-                exponentials(heads[k], s_ps, tb)
-            if tb == 0 and k - 1 in heads:
-                normalize(heads[k - 1])
-            if n < B:
+            if k < len(PARTS):
+                exponentials(parts[k], s_ps, b)
+            if b == 0 and k - 1 in parts:
+                normalize(parts[k - 1])
+            if k < len(PARTS):
                 j = i % BLOCKS
                 if j == 0:
                     ahead = project_steps(n)
@@ -361,13 +385,13 @@ def tile_texttransformer_b_kernel(
             if waiting:
                 step, args = waiting.pop(0)
                 step(*args)
-            if tb == 1 and k - 2 in heads:
-                n2, h2 = divmod(k - 2, NH)
-                weighted_sum(heads[k - 2], n2, h2)
+            if b == 1 and k - 3 in parts:
+                n2, half2, h2 = PARTS[k - 3]
+                weighted_sum(parts[k - 3], n2, half2, h2)
                 if h2 == NH - 1 and n2 != B - 2:
-                    in_next_block(waiting.extend, finish_steps(n2))
-            if (k, tb) == (B * NH - 1, 0):
-                waiting += finish_steps(B - 2)
-            if tb == TB - 1 and k - 1 in heads:
-                turn(heads[k - 1])
+                    in_next_block(waiting.extend, finish_steps(n2, (half2 + 1) * HB))
+            if (k, b) == (len(PARTS) - 2, 0):
+                waiting.extend(finish_steps(B - 2, TB))
+            if b == 1 and k - 2 in parts:
+                turn(parts[k - 2])
         assert not waiting and not due_next

@@ -44,6 +44,7 @@ def tile_texttransformer_b_kernel(
     with (
         tc.tile_pool(name="held", bufs=1) as held,
         tc.tile_pool(name="seq", bufs=2) as seq,
+        tc.tile_pool(name="late", bufs=B) as late,
         tc.tile_pool(name="work", bufs=4) as work,
         tc.psum_pool(name="psum", bufs=BANKS) as psum,
     ):
@@ -94,6 +95,8 @@ def tile_texttransformer_b_kernel(
 
         mean_w = held.tile([P, P], BF16, name="mean_w")
         nc.vector.memset(mean_w[:], 1.0 / D)
+        minus_mean_w = held.tile([P, P], BF16, name="minus_mean_w")
+        nc.vector.memset(minus_mean_w[:], -1.0 / D)
         eps_col = held.tile([P, 1], F32, name="eps_col")
         nc.vector.memset(eps_col[:], EPS)
 
@@ -222,28 +225,19 @@ def tile_texttransformer_b_kernel(
 
         norm = {}
 
-        def sum_of_blocks(blocks):
+        def sum_of_blocks(blocks, pool):
             two_blocks = work.tile([P, CB // 2, T], BF16, name="two_blocks")
             nc.vector.tensor_tensor(
                 two_blocks[:], blocks[:, 0 : CB // 2, :], blocks[:, CB // 2 : CB, :], ALU.add
             )
-            one_block = work.tile([P, T], BF16, name="one_block")
+            one_block = pool.tile([P, T], BF16, name="one_block")
             nc.vector.tensor_tensor(one_block[:], two_blocks[:, 0, :], two_blocks[:, 1, :], ALU.add)
             return one_block
 
-        def center_x0(n):
-            in_next_block(center_matmul, n, sum_of_blocks(x0b[n]))
+        x0_sum = {}
 
-        def center_matmul(n, one_block):
-            mean_ps = psum.tile([P, T], F32, name="mean_ps", tag="bank")
-            nc.tensor.matmul(mean_ps[:], mean_w[:], one_block[:], start=True, stop=True)
-            in_next_block(center_subtract, n, mean_ps)
-
-        def center_subtract(n, mean_ps):
-            for c in range(CB):
-                nc.vector.scalar_tensor_tensor(
-                    x0[n][:, c, :], x0[n][:, c, :], EMB_SCALE, mean_ps[:], ALU.mult, ALU.subtract
-                )
+        def sum_x0(n):
+            x0_sum[n] = sum_of_blocks(x0b[n], late)
 
         def y_of(p, eb):
             n, first, blocks = PIECES[p]
@@ -259,25 +253,31 @@ def tile_texttransformer_b_kernel(
                 nc.tensor.matmul(
                     y_ps[:], weights["o"][:, h, eb * P : (eb + 1) * P],
                     av[n][:, h, first * P : (first + blocks) * P],
-                    start=h == 0, stop=h == NH - 1,
+                    start=h == 0, stop=False,
                 )
+            nc.tensor.matmul(
+                y_ps[:], minus_mean_w[:], x0_sum[n][:, first * P : (first + blocks) * P],
+                start=False, stop=True,
+            )
             in_next_block(residual, p, eb, y_ps)
 
         def residual(p, eb, y_ps):
             nc.vector.scalar_tensor_tensor(
-                y_of(p, eb), y_of(p, eb), bo_centred[:, eb : eb + 1], y_ps[:], ALU.add, ALU.add
+                y_of(p, eb), y_of(p, eb), EMB_SCALE, y_ps[:], ALU.mult, ALU.add
             )
             in_next_block(square, p, eb)
 
         def square(p, eb):
-            nc.scalar.activation(norm[p]["sq"][:, eb, :], y_of(p, eb), ACT.Square)
+            nc.scalar.activation(
+                norm[p]["sq"][:, eb, :], y_of(p, eb), ACT.Square, bias=bo_centred[:, eb : eb + 1]
+            )
             if PIECES[p][0] >= B - 2:
                 in_next_block(var_matmul, p, eb)
             elif eb == CB - 1:
                 in_next_block(sum_of_squares, p)
 
         def sum_of_squares(p):
-            in_next_block(var_of_sum, p, sum_of_blocks(norm[p]["sq"]))
+            in_next_block(var_of_sum, p, sum_of_blocks(norm[p]["sq"], work))
 
         def var_of_sum(p, one_block):
             norm[p]["var_ps"] = psum.tile([P, T], F32, name="var_ps", tag="bank")
@@ -304,7 +304,10 @@ def tile_texttransformer_b_kernel(
         def scale_step(p):
             n, first, blocks = PIECES[p]
             for eb in range(CB):
-                nc.vector.tensor_tensor(y_of(p, eb), y_of(p, eb), norm[p]["rstd"][:], ALU.mult)
+                nc.vector.scalar_tensor_tensor(
+                    y_of(p, eb), y_of(p, eb), bo_centred[:, eb : eb + 1], norm[p]["rstd"][:],
+                    ALU.add, ALU.mult,
+                )
             in_next_block(affine_step, p)
 
         def affine_step(p):
@@ -379,7 +382,7 @@ def tile_texttransformer_b_kernel(
                         look_up(CB - 1, n + 1)
                     if n == 0:
                         waiting.append((center_wo, ()))
-                    waiting.append((center_x0, (n,)))
+                    waiting.append((sum_x0, (n,)))
                 for step, args in ahead[len(GROUPS) * j // BLOCKS : len(GROUPS) * (j + 1) // BLOCKS]:
                     step(*args)
             if waiting:

@@ -313,8 +313,8 @@ def tile_texttransformer_b_kernel(
         def affine_step(p):
             n, first, blocks = PIECES[p]
             for eb in range(CB):
-                nc.scalar.activation(
-                    y_of(p, eb), y_of(p, eb), ACT.Identity, bias=column(4, eb), scale=column(3, eb)
+                nc.vector.tensor_scalar(
+                    y_of(p, eb), y_of(p, eb), column(3, eb), column(4, eb), ALU.mult, ALU.add
                 )
                 nc.sync.dma_start(
                     out[eb * P : (eb + 1) * P, n * T + first * P : n * T + (first + blocks) * P],

@@ -48,6 +48,17 @@ def tile_texttransformer_b_kernel(
         tc.tile_pool(name="work", bufs=4) as work,
         tc.psum_pool(name="psum", bufs=BANKS) as psum,
     ):
+        to_turn = []
+
+        def turn_one():
+            out_block, in_block = to_turn.pop(0)
+            nc.tensor.transpose(out_block, in_block, ident_b[:])
+
+        def matmul(out_ps, lhsT, rhs, start, stop):
+            nc.tensor.matmul(out_ps, lhsT, rhs, start=start, stop=stop)
+            if to_turn:
+                turn_one()
+
         offsets = held.tile([P, B * T // 16], U16, name="offsets")
         nc.sync.dma_start(offsets[:], offs)
 
@@ -103,7 +114,7 @@ def tile_texttransformer_b_kernel(
         bo_b = held.tile([P, CB], BF16, name="bo_b")
         nc.vector.tensor_copy(bo_b[:], vec_cols[:, 2 * CB : 3 * CB])
         bo_ps = psum.tile([P, CB], F32, name="bo_ps", tag="bank")
-        nc.tensor.matmul(bo_ps[:], mean_w[:], bo_b[:], start=True, stop=True)
+        matmul(bo_ps[:], mean_w[:], bo_b[:], start=True, stop=True)
         bo_mean = held.tile([P, 1], F32, name="bo_mean")
         nc.vector.reduce_sum(bo_mean[:], bo_ps[:], axis=AX.X)
         bo_centred = held.tile([P, CB], F32, name="bo_centred")
@@ -145,7 +156,7 @@ def tile_texttransformer_b_kernel(
                 lhsT, rhs = x0b[n][:, c, block], weights["v"][:, c, :]
             else:
                 lhsT, rhs = weights[kind][:, c, block], x0b[n][:, c, :]
-            nc.tensor.matmul(ps[:], lhsT, rhs, start=c == 0, stop=c == CB - 1)
+            matmul(ps[:], lhsT, rhs, start=c == 0, stop=c == CB - 1)
 
         def project_out(ps, n, kind, g):
             dest = qkv[n][kind][:, g, :]
@@ -172,7 +183,7 @@ def tile_texttransformer_b_kernel(
         def scores(n, half, h, b):
             first = half * HT + b * P
             s_ps = psum.tile([P, T], F32, name="s_ps", tag="bank")
-            nc.tensor.matmul(
+            matmul(
                 s_ps[:], qkv[n]["q"][:, h, first : first + P], qkv[n]["k"][:, h, :],
                 start=True, stop=True,
             )
@@ -194,16 +205,22 @@ def tile_texttransformer_b_kernel(
                     part["e"][:, tb, :], part["e"][:, tb, :], recip[:, tb : tb + 1]
                 )
 
-        def turn(part):
-            part["aT"] = work.tile([P, TB, HT], BF16, name="aT")
-            aT_ps = psum.tile([P, TB, HT], BF16, name="aT_ps", tag="bank")
+        def begin_turning(part):
+            part["aT_ps"] = psum.tile([P, TB, HT], BF16, name="aT_ps", tag="bank")
             for tb in range(HB):
                 for ub in range(TB):
-                    nc.tensor.transpose(
-                        aT_ps[:, ub, tb * P : (tb + 1) * P],
-                        part["e"][:, tb, ub * P : (ub + 1) * P], ident_b[:],
+                    to_turn.append(
+                        (
+                            part["aT_ps"][:, ub, tb * P : (tb + 1) * P],
+                            part["e"][:, tb, ub * P : (ub + 1) * P],
+                        )
                     )
-            in_next_block(nc.vector.tensor_copy, part["aT"][:], aT_ps[:])
+
+        def end_turning(part):
+            while to_turn:
+                turn_one()
+            part["aT"] = work.tile([P, TB, HT], BF16, name="aT")
+            in_next_block(nc.vector.tensor_copy, part["aT"][:], part["aT_ps"][:])
 
         av = {}
 
@@ -212,7 +229,7 @@ def tile_texttransformer_b_kernel(
                 av[n] = seq.tile([P, NH, T], BF16, name="av")
             av_ps = psum.tile([P, HT], F32, name="av_ps", tag="bank")
             for ub in range(TB):
-                nc.tensor.matmul(
+                matmul(
                     av_ps[:], qkv[n]["v"][:, ub, h * P : (h + 1) * P], part["aT"][:, ub, :],
                     start=ub == 0, stop=ub == TB - 1,
                 )
@@ -250,12 +267,12 @@ def tile_texttransformer_b_kernel(
                 norm[p] = {"sq": seq.tile([P, CB, width], BF16, name="sq")}
             y_ps = psum.tile([P, width], F32, name="y_ps", tag="bank")
             for h in range(NH):
-                nc.tensor.matmul(
+                matmul(
                     y_ps[:], weights["o"][:, h, eb * P : (eb + 1) * P],
                     av[n][:, h, first * P : (first + blocks) * P],
                     start=h == 0, stop=False,
                 )
-            nc.tensor.matmul(
+            matmul(
                 y_ps[:], minus_mean_w[:], x0_sum[n][:, first * P : (first + blocks) * P],
                 start=False, stop=True,
             )
@@ -281,13 +298,13 @@ def tile_texttransformer_b_kernel(
 
         def var_of_sum(p, one_block):
             norm[p]["var_ps"] = psum.tile([P, T], F32, name="var_ps", tag="bank")
-            nc.tensor.matmul(norm[p]["var_ps"][:], mean_w[:], one_block[:], start=True, stop=True)
+            matmul(norm[p]["var_ps"][:], mean_w[:], one_block[:], start=True, stop=True)
             in_next_block(rstd_step, p)
 
         def var_matmul(p, eb):
             if eb == 0:
                 norm[p]["var_ps"] = psum.tile([P, PIECES[p][2] * P], F32, name="var_ps", tag="bank")
-            nc.tensor.matmul(
+            matmul(
                 norm[p]["var_ps"][:], mean_w[:], norm[p]["sq"][:, eb, :],
                 start=eb == 0, stop=eb == CB - 1,
             )
@@ -374,6 +391,8 @@ def tile_texttransformer_b_kernel(
                 exponentials(parts[k], s_ps, b)
             if b == 0 and k - 1 in parts:
                 normalize(parts[k - 1])
+            if b == 0 and k - 2 in parts:
+                begin_turning(parts[k - 2])
             if k < len(PARTS):
                 j = i % BLOCKS
                 if j == 0:
@@ -396,5 +415,5 @@ def tile_texttransformer_b_kernel(
             if (k, b) == (len(PARTS) - 2, 0):
                 waiting.extend(finish_steps(B - 2, TB))
             if b == 1 and k - 2 in parts:
-                turn(parts[k - 2])
+                end_turning(parts[k - 2])
         assert not waiting and not due_next

@@ -24,7 +24,11 @@ EMB_SCALE = math.sqrt(D)
 
 FLOPS = 2 * D * D * B * T * 4 + 2 * 2 * B * NH * T * T * P
 
-GROUPS = [(kind, g) for g in range(NH) for kind in ("q", "k")] + [("v", g) for g in range(TB)]
+QK_GROUPS = [(kind, g) for g in range(NH) for kind in ("q", "k")]
+V_GROUPS = [("v", g) for g in range(TB)]
+EARLY_GROUPS = [(n, kind, g) for n in range(3) for kind, g in QK_GROUPS[:4]]
+OPEN_GROUPS = EARLY_GROUPS[: BANKS - 2]
+PARKED_BLOCKS = {group: 2 if group[0] == 2 else CB - 1 for group in EARLY_GROUPS[BANKS - 2 :]}
 
 BLOCKS = NH * TB
 HALVES = 2
@@ -43,6 +47,7 @@ def tile_texttransformer_b_kernel(
     nc = tc.nc
     with (
         tc.tile_pool(name="held", bufs=1) as held,
+        tc.tile_pool(name="last_table", bufs=1) as last_table,
         tc.tile_pool(name="seq", bufs=2) as seq,
         tc.tile_pool(name="late", bufs=B) as late,
         tc.tile_pool(name="work", bufs=4) as work,
@@ -69,13 +74,18 @@ def tile_texttransformer_b_kernel(
                 vec_rows[v * CB : (v + 1) * CB, :], vec.rearrange("(b p) o -> b (p o)", p=P)
             )
 
-        weights = {name: held.tile([P, CB, D], BF16, name=f"w{name}") for name in "qkvo"}
+        weights = {name: held.tile([P, CB, D], BF16, name=f"w{name}") for name in "qkv"}
 
-        def load_weights(name, w):
-            nc.sync.dma_start(weights[name][:], w.rearrange("(c p) e -> p c e", p=P))
+        def load_weights(name, w, cols=slice(0, D)):
+            nc.sync.dma_start(
+                weights[name][:, :, cols], w[:, cols].rearrange("(c p) e -> p c e", p=P)
+            )
+
+        first_heads, last_heads = slice(0, D // 2), slice(D // 2, D)
 
         pe_sb = held.tile([P, CB, T], F32, name="pe_sb")
-        table = [held.tile([P, V], F32, name=f"table{c}") for c in range(CB)]
+        table = [held.tile([P, V], F32, name=f"table{c}") for c in range(CB - 1)]
+        table.append(last_table.tile([P, V], F32, name="table_last", tag="bytes"))
         for c in range(CB):
             rows_c = slice(c * P, (c + 1) * P)
             nc.sync.dma_start(pe_sb[:, c, :], pe[rows_c, :])
@@ -84,10 +94,11 @@ def tile_texttransformer_b_kernel(
                 cols_h = slice(half * V // 2, (half + 1) * V // 2)
                 nc.sync.dma_start(table[c][:, cols_h], emb[rows_c, cols_h])
             if c == 0:
-                load_weights("q", wq)
-                load_weights("k", wk)
+                load_weights("q", wq, first_heads)
+                load_weights("k", wk, first_heads)
+        load_weights("q", wq, last_heads)
+        load_weights("k", wk, last_heads)
         load_weights("v", wv)
-        load_weights("o", wo)
 
         ident_f = held.tile([P, P], F32, name="ident_f")
         make_identity(nc, ident_f[:])
@@ -110,6 +121,8 @@ def tile_texttransformer_b_kernel(
         nc.vector.memset(minus_mean_w[:], -1.0 / D)
         eps_col = held.tile([P, 1], F32, name="eps_col")
         nc.vector.memset(eps_col[:], EPS)
+        minus_half = held.tile([P, TB], F32, name="minus_half")
+        nc.vector.memset(minus_half[:], -0.5)
 
         bo_b = held.tile([P, CB], BF16, name="bo_b")
         nc.vector.tensor_copy(bo_b[:], vec_cols[:, 2 * CB : 3 * CB])
@@ -150,16 +163,15 @@ def tile_texttransformer_b_kernel(
         def new_qkv(n):
             qkv[n] = {kind: seq.tile([P, NH, T], BF16, name=kind) for kind in ("q", "k", "v")}
 
-        def project_matmul(ps, n, kind, g, c):
+        def project_matmul(ps, n, kind, g, c, first=0, last=CB - 1):
             block = slice(g * P, (g + 1) * P)
             if kind == "v":
                 lhsT, rhs = x0b[n][:, c, block], weights["v"][:, c, :]
             else:
                 lhsT, rhs = weights[kind][:, c, block], x0b[n][:, c, :]
-            matmul(ps[:], lhsT, rhs, start=c == 0, stop=c == CB - 1)
+            matmul(ps[:], lhsT, rhs, start=c == first, stop=c == last)
 
-        def project_out(ps, n, kind, g):
-            dest = qkv[n][kind][:, g, :]
+        def out_of_psum(dest, ps, kind, g):
             if kind == "q":
                 nc.scalar.activation(
                     dest, ps[:], ACT.Identity, bias=bq_scaled[:, g : g + 1], scale=1.0 / math.sqrt(P)
@@ -167,11 +179,31 @@ def tile_texttransformer_b_kernel(
             else:
                 nc.scalar.copy(dest, ps[:])
 
+        def project_out(ps, n, kind, g):
+            out_of_psum(qkv[n][kind][:, g, :], ps, kind, g)
+
+        parked = {}
+
+        def park_group(n, kind, g):
+            ps = psum.tile([P, T], F32, name="park_ps", tag="bank")
+            blocks = PARKED_BLOCKS[n, kind, g]
+            for c in range(blocks):
+                project_matmul(ps, n, kind, g, c, last=blocks - 1)
+            parked[n, kind, g] = held.tile([P, T], F32, name=f"parked_{kind}{n}{g}")
+            out_of_psum(parked[n, kind, g][:], ps, kind, g)
+
+        def parked_out(ps, n, kind, g):
+            nc.vector.scalar_tensor_tensor(
+                qkv[n][kind][:, g, :], ps[:], 1.0 / math.sqrt(P) if kind == "q" else 1.0,
+                parked[n, kind, g][:], ALU.mult, ALU.add,
+            )
+
         def project_group(n, kind, g):
             ps = psum.tile([P, T], F32, name="proj_ps", tag="bank")
-            for c in range(CB):
-                project_matmul(ps, n, kind, g, c)
-            in_next_block(project_out, ps, n, kind, g)
+            done = PARKED_BLOCKS.get((n, kind, g), 0)
+            for c in range(done, CB):
+                project_matmul(ps, n, kind, g, c, first=done)
+            in_next_block(parked_out if done else project_out, ps, n, kind, g)
 
         def new_part():
             return {
@@ -288,18 +320,45 @@ def tile_texttransformer_b_kernel(
             nc.scalar.activation(
                 norm[p]["sq"][:, eb, :], y_of(p, eb), ACT.Square, bias=bo_centred[:, eb : eb + 1]
             )
-            if PIECES[p][0] >= B - 2:
+            if p == len(PIECES) - 1:
                 in_next_block(var_matmul, p, eb)
             elif eb == CB - 1:
-                in_next_block(sum_of_squares, p)
+                in_next_block(var_columns, p)
 
-        def sum_of_squares(p):
-            in_next_block(var_of_sum, p, sum_of_blocks(norm[p]["sq"], work))
+        def var_columns(p):
+            blocks = PIECES[p][2]
+            norm[p]["var"] = psum.tile([P, blocks], F32, name="var_cols", tag="bank")
+            for b in range(blocks):
+                for eb in range(CB):
+                    nc.tensor.matmul(
+                        norm[p]["var"][:, b : b + 1],
+                        norm[p]["sq"][:, eb, b * P : (b + 1) * P], mean_w[:, 0:1],
+                        start=eb == 0, stop=eb == CB - 1,
+                    )
+            in_next_block(rstd_columns, p)
 
-        def var_of_sum(p, one_block):
-            norm[p]["var_ps"] = psum.tile([P, T], F32, name="var_ps", tag="bank")
-            matmul(norm[p]["var_ps"][:], mean_w[:], one_block[:], start=True, stop=True)
-            in_next_block(rstd_step, p)
+        def rstd_columns(p):
+            blocks = PIECES[p][2]
+            var = work.tile([P, blocks], F32, name="var")
+            nc.vector.tensor_scalar_add(var[:], norm[p]["var"][:], EPS)
+            cols = work.tile([P, blocks], F32, name="rstd_cols")
+            nc.gpsimd.tensor_tensor(cols[:], var[:], minus_half[:, 0:blocks], ALU.pow)
+            in_next_block(widen_rstd, p, cols)
+
+        def widen_rstd(p, cols):
+            blocks = PIECES[p][2]
+            wide = work.tile([P, blocks, P], F32, name="rstd_wide")
+            nc.vector.tensor_copy(wide[:], cols[:].unsqueeze(2).to_broadcast([P, blocks, P]))
+            in_next_block(rstd_rows, p, wide)
+
+        def rstd_rows(p, wide):
+            blocks = PIECES[p][2]
+            norm[p]["rstd"] = psum.tile([P, blocks * P], F32, name="rstd_rows", tag="bank")
+            for b in range(blocks):
+                nc.tensor.transpose(
+                    norm[p]["rstd"][:, b * P : (b + 1) * P], wide[:, b, :], ident_f[:]
+                )
+            in_next_block(scale_step, p)
 
         def var_matmul(p, eb):
             if eb == 0:
@@ -347,35 +406,42 @@ def tile_texttransformer_b_kernel(
             ]
 
         def project_steps(n):
-            steps = [(project_group, (n, kind, g)) for kind, g in GROUPS[BANKS:]]
+            groups = [(n, kind, g) for kind, g in V_GROUPS]
+            if n == 0:
+                groups = [(0, kind, g) for kind, g in QK_GROUPS[NH:]] + groups
             if n + 1 < B:
-                new_qkv(n + 1)
-                steps += [(project_group, (n + 1, kind, g)) for kind, g in GROUPS[:BANKS]]
-            return steps
+                if n + 1 not in qkv:
+                    new_qkv(n + 1)
+                groups += [
+                    (n + 1, kind, g) for kind, g in QK_GROUPS if (n + 1, kind, g) not in OPEN_GROUPS
+                ]
+            return [(project_group, args) for args in groups]
 
-        new_qkv(0)
-        first_ps = [psum.tile([P, T], F32, name=f"first_ps{i}", tag="bank") for i in range(BANKS)]
+        for n in range(2):
+            new_qkv(n)
+        open_ps = {
+            (n, kind, g): psum.tile([P, T], F32, name=f"open_{kind}{n}{g}", tag="bank")
+            for n, kind, g in OPEN_GROUPS
+        }
         for c in range(CB - 1):
             for n in range(B):
                 look_up(c, n)
-            for ps, (kind, g) in zip(first_ps, GROUPS):
-                project_matmul(ps, 0, kind, g, c)
+            for group in OPEN_GROUPS:
+                project_matmul(open_ps[group], *group, c)
+            for group in [group for group, blocks in PARKED_BLOCKS.items() if blocks == c + 1]:
+                park_group(*group)
         look_up(CB - 1, 0)
+        for group in OPEN_GROUPS[:2]:
+            project_matmul(open_ps[group], *group, CB - 1)
+            project_out(open_ps[group], *group)
+        to_close = OPEN_GROUPS[2:]
 
-        def close_group(ps, kind, g):
-            project_matmul(ps, 0, kind, g, CB - 1)
-            project_out(ps, 0, kind, g)
-
-        def close_group_later(ps, kind, g):
-            project_matmul(ps, 0, kind, g, CB - 1)
-            in_next_block(project_out, ps, 0, kind, g)
-
-        open_groups = [(close_group_later, (ps, kind, g)) for ps, (kind, g) in zip(first_ps, GROUPS)]
-        for step, args in open_groups[:4]:
-            close_group(*args)
+        def close_group(group):
+            project_matmul(open_ps[group], *group, CB - 1)
+            in_next_block(project_out, open_ps[group], *group)
 
         parts = {}
-        waiting = open_groups[4:]
+        waiting = []
         for i in range((len(PARTS) + 3) * HB + DRAIN):
             k, b = divmod(i, HB)
             if k < len(PARTS):
@@ -397,12 +463,21 @@ def tile_texttransformer_b_kernel(
                 j = i % BLOCKS
                 if j == 0:
                     ahead = project_steps(n)
-                    if n + 1 < B:
-                        look_up(CB - 1, n + 1)
-                    if n == 0:
-                        waiting.append((center_wo, ()))
                     waiting.append((sum_x0, (n,)))
-                for step, args in ahead[len(GROUPS) * j // BLOCKS : len(GROUPS) * (j + 1) // BLOCKS]:
+                if n == 0 and j + 1 < B:
+                    look_up(CB - 1, j + 1)
+                elif n == 0 and j + 1 == B:
+                    weights["o"] = last_table.tile([P, CB, D], BF16, name="wo_sb", tag="bytes")
+                    load_weights("o", wo)
+                    waiting.append((center_wo, ()))
+                for group in to_close[:2]:
+                    close_group(group)
+                to_close = to_close[2:]
+                if n == 0:
+                    now = ahead[j + 1 : j + 2] if j else ahead[:2]
+                else:
+                    now = ahead[12 * j // BLOCKS : 12 * (j + 1) // BLOCKS]
+                for step, args in now:
                     step(*args)
             if waiting:
                 step, args = waiting.pop(0)

@@ -26,9 +26,10 @@ FLOPS = 2 * D * D * B * T * 4 + 2 * 2 * B * NH * T * T * P
 
 QK_GROUPS = [(kind, g) for g in range(NH) for kind in ("q", "k")]
 V_GROUPS = [("v", g) for g in range(TB)]
-EARLY_GROUPS = [(n, kind, g) for n in range(3) for kind, g in QK_GROUPS[:4]]
-OPEN_GROUPS = EARLY_GROUPS[: BANKS - 2]
-PARKED_BLOCKS = {group: 2 if group[0] == 2 else CB - 1 for group in EARLY_GROUPS[BANKS - 2 :]}
+EARLY_GROUPS = {n: [(n, kind, g) for kind, g in QK_GROUPS[:4]] for n in range(B)}
+OPEN_GROUPS = EARLY_GROUPS[0] + EARLY_GROUPS[1]
+PARKED_GROUPS = EARLY_GROUPS[2] + EARLY_GROUPS[3]
+PARKED_BLOCKS = 2
 
 BLOCKS = NH * TB
 HALVES = 2
@@ -144,14 +145,22 @@ def tile_texttransformer_b_kernel(
                 )
 
         x0 = [held.tile([P, CB, T], F32, name=f"x0_{n}") for n in range(B)]
-        x0b = [held.tile([P, CB, T], BF16, name=f"x0b_{n}") for n in range(B)]
+        x0b_low = [held.tile([P, CB // 2, T], BF16, name=f"x0b_low{n}") for n in range(B)]
+        x0b_high = {}
+
+        def x0b(n, c):
+            return x0b_low[n][:, c, :] if c < CB // 2 else x0b_high[n][:, c - CB // 2, :]
 
         def look_up(c, n):
             piece = offsets[:, n * T // 16 : (n + 1) * T // 16]
             nc.vector.tensor_tensor(
                 x0[n][:, c, :], table[c][:].indirect(piece), pe_sb[:, c, :], ALU.add
             )
-            nc.scalar.mul(x0b[n][:, c, :], x0[n][:, c, :], EMB_SCALE)
+
+        def round_x0(c, n):
+            if c == CB // 2:
+                x0b_high[n] = seq.tile([P, CB // 2, T], BF16, name="x0b_high")
+            nc.scalar.mul(x0b(n, c), x0[n][:, c, :], EMB_SCALE)
 
         due_next = []
 
@@ -166,9 +175,9 @@ def tile_texttransformer_b_kernel(
         def project_matmul(ps, n, kind, g, c, first=0, last=CB - 1):
             block = slice(g * P, (g + 1) * P)
             if kind == "v":
-                lhsT, rhs = x0b[n][:, c, block], weights["v"][:, c, :]
+                lhsT, rhs = x0b(n, c)[:, block], weights["v"][:, c, :]
             else:
-                lhsT, rhs = weights[kind][:, c, block], x0b[n][:, c, :]
+                lhsT, rhs = weights[kind][:, c, block], x0b(n, c)
             matmul(ps[:], lhsT, rhs, start=c == first, stop=c == last)
 
         def out_of_psum(dest, ps, kind, g):
@@ -186,9 +195,8 @@ def tile_texttransformer_b_kernel(
 
         def park_group(n, kind, g):
             ps = psum.tile([P, T], F32, name="park_ps", tag="bank")
-            blocks = PARKED_BLOCKS[n, kind, g]
-            for c in range(blocks):
-                project_matmul(ps, n, kind, g, c, last=blocks - 1)
+            for c in range(PARKED_BLOCKS):
+                project_matmul(ps, n, kind, g, c, last=PARKED_BLOCKS - 1)
             parked[n, kind, g] = held.tile([P, T], F32, name=f"parked_{kind}{n}{g}")
             out_of_psum(parked[n, kind, g][:], ps, kind, g)
 
@@ -200,7 +208,7 @@ def tile_texttransformer_b_kernel(
 
         def project_group(n, kind, g):
             ps = psum.tile([P, T], F32, name="proj_ps", tag="bank")
-            done = PARKED_BLOCKS.get((n, kind, g), 0)
+            done = PARKED_BLOCKS if (n, kind, g) in PARKED_GROUPS else 0
             for c in range(done, CB):
                 project_matmul(ps, n, kind, g, c, first=done)
             in_next_block(parked_out if done else project_out, ps, n, kind, g)
@@ -274,19 +282,13 @@ def tile_texttransformer_b_kernel(
 
         norm = {}
 
-        def sum_of_blocks(blocks, pool):
-            two_blocks = work.tile([P, CB // 2, T], BF16, name="two_blocks")
-            nc.vector.tensor_tensor(
-                two_blocks[:], blocks[:, 0 : CB // 2, :], blocks[:, CB // 2 : CB, :], ALU.add
-            )
-            one_block = pool.tile([P, T], BF16, name="one_block")
-            nc.vector.tensor_tensor(one_block[:], two_blocks[:, 0, :], two_blocks[:, 1, :], ALU.add)
-            return one_block
-
         x0_sum = {}
 
         def sum_x0(n):
-            x0_sum[n] = sum_of_blocks(x0b[n], late)
+            pair = work.tile([P, CB // 2, T], BF16, name="pair")
+            nc.vector.tensor_tensor(pair[:], x0b_low[n][:], x0b_high[n][:], ALU.add)
+            x0_sum[n] = late.tile([P, T], BF16, name="x0_sum")
+            nc.vector.tensor_tensor(x0_sum[n][:], pair[:, 0, :], pair[:, 1, :], ALU.add)
 
         def y_of(p, eb):
             n, first, blocks = PIECES[p]
@@ -348,7 +350,7 @@ def tile_texttransformer_b_kernel(
         def widen_rstd(p, cols):
             blocks = PIECES[p][2]
             wide = work.tile([P, blocks, P], F32, name="rstd_wide")
-            nc.vector.tensor_copy(wide[:], cols[:].unsqueeze(2).to_broadcast([P, blocks, P]))
+            nc.gpsimd.tensor_copy(wide[:], cols[:].unsqueeze(2).to_broadcast([P, blocks, P]))
             in_next_block(rstd_rows, p, wide)
 
         def rstd_rows(p, wide):
@@ -389,9 +391,15 @@ def tile_texttransformer_b_kernel(
         def affine_step(p):
             n, first, blocks = PIECES[p]
             for eb in range(CB):
-                nc.vector.tensor_scalar(
-                    y_of(p, eb), y_of(p, eb), column(3, eb), column(4, eb), ALU.mult, ALU.add
-                )
+                if n < B - 2:
+                    nc.vector.tensor_scalar(
+                        y_of(p, eb), y_of(p, eb), column(3, eb), column(4, eb), ALU.mult, ALU.add
+                    )
+                else:
+                    nc.scalar.activation(
+                        y_of(p, eb), y_of(p, eb), ACT.Identity,
+                        bias=column(4, eb), scale=column(3, eb),
+                    )
                 nc.sync.dma_start(
                     out[eb * P : (eb + 1) * P, n * T + first * P : n * T + (first + blocks) * P],
                     y_of(p, eb),
@@ -419,18 +427,27 @@ def tile_texttransformer_b_kernel(
 
         for n in range(2):
             new_qkv(n)
-        open_ps = {
-            (n, kind, g): psum.tile([P, T], F32, name=f"open_{kind}{n}{g}", tag="bank")
-            for n, kind, g in OPEN_GROUPS
-        }
+        open_ps = {}
+
+        def add_to_open(n, c):
+            for group in EARLY_GROUPS[n]:
+                if c == 0:
+                    open_ps[group] = psum.tile([P, T], F32, name="open_ps", tag="bank")
+                project_matmul(open_ps[group], *group, c)
+
         for c in range(CB - 1):
             for n in range(B):
                 look_up(c, n)
-            for group in OPEN_GROUPS:
-                project_matmul(open_ps[group], *group, c)
-            for group in [group for group, blocks in PARKED_BLOCKS.items() if blocks == c + 1]:
-                park_group(*group)
+                if c < CB // 2 or n < 2:
+                    round_x0(c, n)
+            add_to_open(0, c)
+            if c == PARKED_BLOCKS - 1:
+                for group in PARKED_GROUPS:
+                    park_group(*group)
+        for c in range(CB - 1):
+            add_to_open(1, c)
         look_up(CB - 1, 0)
+        round_x0(CB - 1, 0)
         for group in OPEN_GROUPS[:2]:
             project_matmul(open_ps[group], *group, CB - 1)
             project_out(open_ps[group], *group)
@@ -455,21 +472,29 @@ def tile_texttransformer_b_kernel(
                 step(*args)
             if k < len(PARTS):
                 exponentials(parts[k], s_ps, b)
+            if (k, b) == (len(PARTS) - 1, HB - 1):
+                early = work.tile([P, 1], F32, name="early")
+                nc.scalar.activation(
+                    early[:], parts[k]["e_sum"][:, b : b + 1], ACT.Abs_reciprocal_sqrt
+                )
             if b == 0 and k - 1 in parts:
                 normalize(parts[k - 1])
             if b == 0 and k - 2 in parts:
                 begin_turning(parts[k - 2])
             if k < len(PARTS):
                 j = i % BLOCKS
-                if j == 0:
-                    ahead = project_steps(n)
-                    waiting.append((sum_x0, (n,)))
                 if n == 0 and j + 1 < B:
                     look_up(CB - 1, j + 1)
                 elif n == 0 and j + 1 == B:
                     weights["o"] = last_table.tile([P, CB, D], BF16, name="wo_sb", tag="bytes")
                     load_weights("o", wo)
                     waiting.append((center_wo, ()))
+                if j == 0:
+                    ahead = project_steps(n)
+                    waiting.append((sum_x0, (n,)))
+                    if n + 1 < B:
+                        for c in range(CB // 2 if n else CB - 1, CB):
+                            round_x0(c, n + 1)
                 for group in to_close[:2]:
                     close_group(group)
                 to_close = to_close[2:]

@@ -39,7 +39,10 @@ HT = HB * P
 PARTS = [(n, half, h) for n in range(B) for half in range(HALVES) for h in range(NH)]
 DRAIN = 20
 
-PIECES = [(n, 0, TB) for n in range(B - 1)] + [(B - 1, 0, TB // 2), (B - 1, TB // 2, TB // 2)]
+PIECES = [(n, 0, TB) for n in range(B - 1)] + [
+    (B - 1, 0, TB // 2), (B - 1, TB // 2, TB // 4), (B - 1, TB - TB // 4, TB // 4)
+]
+FIRST_LATE_PIECE = len(PIECES) - 2
 
 
 def tile_texttransformer_b_kernel(
@@ -322,10 +325,8 @@ def tile_texttransformer_b_kernel(
             nc.scalar.activation(
                 norm[p]["sq"][:, eb, :], y_of(p, eb), ACT.Square, bias=bo_centred[:, eb : eb + 1]
             )
-            if p == len(PIECES) - 1:
-                in_next_block(var_matmul, p, eb)
-            elif eb == CB - 1:
-                in_next_block(var_columns, p)
+            if eb == CB - 1:
+                in_next_block(var_rows if p >= FIRST_LATE_PIECE else var_columns, p)
 
         def var_columns(p):
             blocks = PIECES[p][2]
@@ -345,37 +346,31 @@ def tile_texttransformer_b_kernel(
             nc.vector.tensor_scalar_add(var[:], norm[p]["var"][:], EPS)
             cols = work.tile([P, blocks], F32, name="rstd_cols")
             nc.gpsimd.tensor_tensor(cols[:], var[:], minus_half[:, 0:blocks], ALU.pow)
-            in_next_block(widen_rstd, p, cols)
+            in_next_block(rstd_rows, p, cols)
 
-        def widen_rstd(p, cols):
-            blocks = PIECES[p][2]
-            wide = work.tile([P, blocks, P], F32, name="rstd_wide")
-            nc.gpsimd.tensor_copy(wide[:], cols[:].unsqueeze(2).to_broadcast([P, blocks, P]))
-            in_next_block(rstd_rows, p, wide)
-
-        def rstd_rows(p, wide):
+        def rstd_rows(p, cols):
             blocks = PIECES[p][2]
             norm[p]["rstd"] = psum.tile([P, blocks * P], F32, name="rstd_rows", tag="bank")
             for b in range(blocks):
                 nc.tensor.transpose(
-                    norm[p]["rstd"][:, b * P : (b + 1) * P], wide[:, b, :], ident_f[:]
+                    norm[p]["rstd"][:, b * P : (b + 1) * P],
+                    cols[:, b : b + 1].to_broadcast([P, P]), ident_f[:],
                 )
             in_next_block(scale_step, p)
 
-        def var_matmul(p, eb):
-            if eb == 0:
-                norm[p]["var_ps"] = psum.tile([P, PIECES[p][2] * P], F32, name="var_ps", tag="bank")
-            matmul(
-                norm[p]["var_ps"][:], mean_w[:], norm[p]["sq"][:, eb, :],
-                start=eb == 0, stop=eb == CB - 1,
-            )
-            if eb == CB - 1:
-                in_next_block(rstd_step, p)
+        def var_rows(p):
+            norm[p]["var"] = psum.tile([P, PIECES[p][2] * P], F32, name="var_rows", tag="bank")
+            for eb in range(CB):
+                matmul(
+                    norm[p]["var"][:], mean_w[:], norm[p]["sq"][:, eb, :],
+                    start=eb == 0, stop=eb == CB - 1,
+                )
+            in_next_block(rstd_step, p)
 
         def rstd_step(p):
             norm[p]["rstd"] = seq.tile([P, PIECES[p][2] * P], F32, name="rstd")
             nc.scalar.activation(
-                norm[p]["rstd"][:], norm[p]["var_ps"][:], ACT.Abs_reciprocal_sqrt, bias=eps_col[:]
+                norm[p]["rstd"][:], norm[p]["var"][:], ACT.Abs_reciprocal_sqrt, bias=eps_col[:]
             )
             in_next_block(scale_step, p)
 
@@ -408,8 +403,8 @@ def tile_texttransformer_b_kernel(
         def finish_steps(n, blocks_done):
             return [
                 (wo_step, (p, eb))
-                for p in range(len(PIECES))
-                if (n, blocks_done) == (PIECES[p][0], PIECES[p][1] + PIECES[p][2])
+                for p, (piece_n, first, blocks) in enumerate(PIECES)
+                if piece_n == n and blocks_done - HB < first + blocks <= blocks_done
                 for eb in range(CB)
             ]
 
@@ -504,9 +499,10 @@ def tile_texttransformer_b_kernel(
                     now = ahead[12 * j // BLOCKS : 12 * (j + 1) // BLOCKS]
                 for step, args in now:
                     step(*args)
-            if waiting:
-                step, args = waiting.pop(0)
-                step(*args)
+            for turn in range(1 if k < len(PARTS) + 3 else 2):
+                if waiting:
+                    step, args = waiting.pop(0)
+                    step(*args)
             if b == 1 and k - 3 in parts:
                 n2, half2, h2 = PARTS[k - 3]
                 weighted_sum(parts[k - 3], n2, half2, h2)

@@ -71,21 +71,19 @@ def tile_texttransformer_b_kernel(
         offsets = held.tile([P, B * T // 16], U16, name="offsets")
         nc.sync.dma_start(offsets[:], offs)
 
-        vec_rows = held.tile([P, P], F32, name="vec_rows")
-        nc.vector.memset(vec_rows[:], 0.0)
-        for v, vec in enumerate((bq, bv, bo, gain, shift)):
-            nc.sync.dma_start(
-                vec_rows[v * CB : (v + 1) * CB, :], vec.rearrange("(b p) o -> b (p o)", p=P)
-            )
-
         weights = {name: held.tile([P, CB, D], BF16, name=f"w{name}") for name in "qkv"}
 
-        def load_weights(name, w, cols=slice(0, D)):
-            nc.sync.dma_start(
+        def load_weights(queue, name, w, cols=slice(0, D)):
+            queue.dma_start(
                 weights[name][:, :, cols], w[:, cols].rearrange("(c p) e -> p c e", p=P)
             )
 
         first_heads, last_heads = slice(0, D // 2), slice(D // 2, D)
+        load_weights(nc.scalar, "q", wq, first_heads)
+        load_weights(nc.scalar, "k", wk, first_heads)
+
+        vec_rows = held.tile([P, P], F32, name="vec_rows")
+        nc.vector.memset(vec_rows[:], 0.0)
 
         pe_sb = held.tile([P, CB, T], F32, name="pe_sb")
         table = [held.tile([P, V], F32, name=f"table{c}") for c in range(CB - 1)]
@@ -98,11 +96,13 @@ def tile_texttransformer_b_kernel(
                 cols_h = slice(half * V // 2, (half + 1) * V // 2)
                 nc.sync.dma_start(table[c][:, cols_h], emb[rows_c, cols_h])
             if c == 0:
-                load_weights("q", wq, first_heads)
-                load_weights("k", wk, first_heads)
-        load_weights("q", wq, last_heads)
-        load_weights("k", wk, last_heads)
-        load_weights("v", wv)
+                for v, vec in enumerate((bq, bv, bo, gain, shift)):
+                    nc.sync.dma_start(
+                        vec_rows[v * CB : (v + 1) * CB, :], vec.rearrange("(b p) o -> b (p o)", p=P)
+                    )
+        load_weights(nc.sync, "q", wq, last_heads)
+        load_weights(nc.sync, "k", wk, last_heads)
+        load_weights(nc.sync, "v", wv)
 
         ident_f = held.tile([P, P], F32, name="ident_f")
         make_identity(nc, ident_f[:])
@@ -482,7 +482,7 @@ def tile_texttransformer_b_kernel(
                     look_up(CB - 1, j + 1)
                 elif n == 0 and j + 1 == B:
                     weights["o"] = last_table.tile([P, CB, D], BF16, name="wo_sb", tag="bytes")
-                    load_weights("o", wo)
+                    load_weights(nc.sync, "o", wo)
                     waiting.append((center_wo, ()))
                 if j == 0:
                     ahead = project_steps(n)

@@ -88,10 +88,17 @@ def tile_texttransformer_b_kernel(
         pe_sb = held.tile([P, CB, T], F32, name="pe_sb")
         table = [held.tile([P, V], F32, name=f"table{c}") for c in range(CB - 1)]
         table.append(last_table.tile([P, V], F32, name="table_last", tag="bytes"))
+
+        def load_pe(c):
+            nc.sync.dma_start(pe_sb[:, c, :], pe[c * P : (c + 1) * P, :])
+            nc.scalar.mul(pe_sb[:, c, :], pe_sb[:, c, :], 1.0 / EMB_SCALE)
+
         for c in range(CB):
             rows_c = slice(c * P, (c + 1) * P)
-            nc.sync.dma_start(pe_sb[:, c, :], pe[rows_c, :])
-            nc.scalar.mul(pe_sb[:, c, :], pe_sb[:, c, :], 1.0 / EMB_SCALE)
+            if c < CB - 1:
+                load_pe(c)
+            if c == CB - 2:
+                load_pe(CB - 1)
             for half in range(2):
                 cols_h = slice(half * V // 2, (half + 1) * V // 2)
                 nc.sync.dma_start(table[c][:, cols_h], emb[rows_c, cols_h])
@@ -128,14 +135,15 @@ def tile_texttransformer_b_kernel(
         minus_half = held.tile([P, TB], F32, name="minus_half")
         nc.vector.memset(minus_half[:], -0.5)
 
-        bo_b = held.tile([P, CB], BF16, name="bo_b")
-        nc.vector.tensor_copy(bo_b[:], vec_cols[:, 2 * CB : 3 * CB])
-        bo_ps = psum.tile([P, CB], F32, name="bo_ps", tag="bank")
-        matmul(bo_ps[:], mean_w[:], bo_b[:], start=True, stop=True)
-        bo_mean = held.tile([P, 1], F32, name="bo_mean")
-        nc.vector.reduce_sum(bo_mean[:], bo_ps[:], axis=AX.X)
         bo_centred = held.tile([P, CB], F32, name="bo_centred")
-        nc.vector.tensor_scalar_sub(bo_centred[:], vec_cols[:, 2 * CB : 3 * CB], bo_mean[:])
+
+        def center_bo(bo_b):
+            nc.vector.tensor_copy(bo_b, vec_cols[:, 2 * CB : 3 * CB])
+            bo_ps = psum.tile([P, CB], F32, name="bo_ps", tag="bank")
+            matmul(bo_ps[:], mean_w[:], bo_b, start=True, stop=True)
+            bo_mean = held.tile([P, 1], F32, name="bo_mean")
+            nc.vector.reduce_sum(bo_mean[:], bo_ps[:], axis=AX.X)
+            nc.vector.tensor_scalar_sub(bo_centred[:], vec_cols[:, 2 * CB : 3 * CB], bo_mean[:])
 
         def center_wo():
             row_mean = held.tile([P, CB], F32, name="row_mean")
@@ -481,9 +489,11 @@ def tile_texttransformer_b_kernel(
                 if n == 0 and j + 1 < B:
                     look_up(CB - 1, j + 1)
                 elif n == 0 and j + 1 == B:
-                    weights["o"] = last_table.tile([P, CB, D], BF16, name="wo_sb", tag="bytes")
+                    late_bytes = last_table.tile([P, CB + 1, D], BF16, name="late_bytes", tag="bytes")
+                    weights["o"] = late_bytes[:, 0:CB, :]
                     load_weights(nc.sync, "o", wo)
                     waiting.append((center_wo, ()))
+                    waiting.append((center_bo, (late_bytes[:, CB, 0:CB],)))
                 if j == 0:
                     ahead = project_steps(n)
                     waiting.append((sum_x0, (n,)))

@@ -88,17 +88,10 @@ def tile_texttransformer_b_kernel(
         pe_sb = held.tile([P, CB, T], F32, name="pe_sb")
         table = [held.tile([P, V], F32, name=f"table{c}") for c in range(CB - 1)]
         table.append(last_table.tile([P, V], F32, name="table_last", tag="bytes"))
-
-        def load_pe(c):
-            nc.sync.dma_start(pe_sb[:, c, :], pe[c * P : (c + 1) * P, :])
-            nc.scalar.mul(pe_sb[:, c, :], pe_sb[:, c, :], 1.0 / EMB_SCALE)
-
         for c in range(CB):
             rows_c = slice(c * P, (c + 1) * P)
-            if c < CB - 1:
-                load_pe(c)
-            if c == CB - 2:
-                load_pe(CB - 1)
+            nc.sync.dma_start(pe_sb[:, c, :], pe[rows_c, :])
+            nc.scalar.mul(pe_sb[:, c, :], pe_sb[:, c, :], 1.0 / EMB_SCALE)
             for half in range(2):
                 cols_h = slice(half * V // 2, (half + 1) * V // 2)
                 nc.sync.dma_start(table[c][:, cols_h], emb[rows_c, cols_h])

import math

import concourse.mybir as mybir
from concourse.masks import make_identity

F32 = mybir.dt.float32
BF16 = mybir.dt.bfloat16
U16 = mybir.dt.uint16
ALU = mybir.AluOpType
ACT = mybir.ActivationFunctionType
AX = mybir.AxisListType

P = 128
V = 4096
D = 512
NH = 4
B = 4
T = 512
CB = D // P
TB = T // P
BANKS = 8
EPS = 1e-6
EMB_SCALE = math.sqrt(D)

FLOPS = 2 * D * D * B * T * 4 + 2 * 2 * B * NH * T * T * P

QK_GROUPS = [(kind, g) for g in range(NH) for kind in ("q", "k")]
V_GROUPS = [("v", g) for g in range(TB)]
EARLY_GROUPS = {n: [(n, kind, g) for kind, g in QK_GROUPS[:4]] for n in range(B)}
OPEN_GROUPS = EARLY_GROUPS[0] + EARLY_GROUPS[1]
PARKED_GROUPS = EARLY_GROUPS[2] + EARLY_GROUPS[3]
PARKED_BLOCKS = 2

BLOCKS = NH * TB
HALVES = 2
HB = TB // HALVES
HT = HB * P

PARTS = [(n, half, h) for n in range(B) for half in range(HALVES) for h in range(NH)]
DRAIN = 20

PIECES = [(n, 0, TB) for n in range(B - 1)] + [
    (B - 1, 0, TB // 2), (B - 1, TB // 2, TB // 4), (B - 1, TB - TB // 4, TB // 4)
]
FIRST_LATE_PIECE = len(PIECES) - 2


def tile_texttransformer_b_kernel(
    tc, emb, pe, wq, bq, wk, wv, bv, wo, bo, gain, shift, offs, out
):
    nc = tc.nc
    with (
        tc.tile_pool(name="held", bufs=1) as held,
        tc.tile_pool(name="last_table", bufs=1) as last_table,
        tc.tile_pool(name="seq", bufs=2) as seq,
        tc.tile_pool(name="late", bufs=B) as late,
        tc.tile_pool(name="work", bufs=4) as work,
        tc.psum_pool(name="psum", bufs=BANKS) as psum,
    ):
        to_turn = []

        def turn_one():
            out_block, in_block = to_turn.pop(0)
            nc.tensor.transpose(out_block, in_block, ident_b[:])

        def matmul(out_ps, lhsT, rhs, start, stop):
            nc.tensor.matmul(out_ps, lhsT, rhs, start=start, stop=stop)
            if to_turn:
                turn_one()

        offsets = held.tile([P, B * T // 16], U16, name="offsets")
        nc.sync.dma_start(offsets[:], offs)

        weights = {name: held.tile([P, CB, D], BF16, name=f"w{name}") for name in "qkv"}

        def load_weights(queue, name, w, cols=slice(0, D)):
            queue.dma_start(
                weights[name][:, :, cols], w[:, cols].rearrange("(c p) e -> p c e", p=P)
            )

        first_heads, last_heads = slice(0, D // 2), slice(D // 2, D)
        load_weights(nc.scalar, "q", wq, first_heads)
        load_weights(nc.scalar, "k", wk, first_heads)

        vec_rows = held.tile([P, P], F32, name="vec_rows")
        nc.vector.memset(vec_rows[:], 0.0)

        pe_sb = held.tile([P, CB, T], F32, name="pe_sb")
        table = [held.tile([P, V], F32, name=f"table{c}") for c in range(CB - 1)]
        table.append(last_table.tile([P, V], F32, name="table_last", tag="bytes"))
        for c in range(CB):
            rows_c = slice(c * P, (c + 1) * P)
            nc.sync.dma_start(pe_sb[:, c, :], pe[rows_c, :])
            nc.scalar.mul(pe_sb[:, c, :], pe_sb[:, c, :], 1.0 / EMB_SCALE)
            for half in range(2):
                cols_h = slice(half * V // 2, (half + 1) * V // 2)
                nc.sync.dma_start(table[c][:, cols_h], emb[rows_c, cols_h])
            if c == 0:
                for v, vec in enumerate((bq, bv, bo, gain, shift)):
                    nc.sync.dma_start(
                        vec_rows[v * CB : (v + 1) * CB, :], vec.rearrange("(b p) o -> b (p o)", p=P)
                    )
        load_weights(nc.sync, "q", wq, last_heads)
        load_weights(nc.sync, "k", wk, last_heads)
        load_weights(nc.sync, "v", wv)

        ident_f = held.tile([P, P], F32, name="ident_f")
        make_identity(nc, ident_f[:])
        ident_b = held.tile([P, P], BF16, name="ident_b")
        make_identity(nc, ident_b[:])
        vec_ps = psum.tile([P, P], F32, name="vec_ps", tag="bank")
        nc.tensor.transpose(vec_ps[:], vec_rows[:], ident_f[:])
        vec_cols = held.tile([P, 5 * CB], F32, name="vec_cols")
        nc.vector.tensor_copy(vec_cols[:], vec_ps[:, 0 : 5 * CB])

        def column(v, b):
            return vec_cols[:, v * CB + b : v * CB + b + 1]

        bq_scaled = held.tile([P, NH], F32, name="bq_scaled")
        nc.vector.tensor_scalar_mul(bq_scaled[:], vec_cols[:, 0:NH], 1.0 / math.sqrt(P))

        mean_w = held.tile([P, P], BF16, name="mean_w")
        nc.vector.memset(mean_w[:], 1.0 / D)
        minus_mean_w = held.tile([P, P], BF16, name="minus_mean_w")
        nc.vector.memset(minus_mean_w[:], -1.0 / D)
        eps_col = held.tile([P, 1], F32, name="eps_col")
        nc.vector.memset(eps_col[:], EPS)
        minus_half = held.tile([P, TB], F32, name="minus_half")
        nc.vector.memset(minus_half[:], -0.5)

        bo_centred = held.tile([P, CB], F32, name="bo_centred")

        def center_bo(bo_b):
            nc.vector.tensor_copy(bo_b, vec_cols[:, 2 * CB : 3 * CB])
            bo_ps = psum.tile([P, CB], F32, name="bo_ps", tag="bank")
            matmul(bo_ps[:], mean_w[:], bo_b, start=True, stop=True)
            bo_mean = held.tile([P, 1], F32, name="bo_mean")
            nc.vector.reduce_sum(bo_mean[:], bo_ps[:], axis=AX.X)
            nc.vector.tensor_scalar_sub(bo_centred[:], vec_cols[:, 2 * CB : 3 * CB], bo_mean[:])

        def center_wo():
            row_mean = held.tile([P, CB], F32, name="row_mean")
            for c in range(CB):
                nc.vector.reduce_sum(row_mean[:, c : c + 1], weights["o"][:, c, :], axis=AX.X)
            nc.vector.tensor_scalar_mul(row_mean[:], row_mean[:], 1.0 / D)
            for c in range(CB):
                nc.vector.tensor_scalar_sub(
                    weights["o"][:, c, :], weights["o"][:, c, :], row_mean[:, c : c + 1]
                )

        x0 = [held.tile([P, CB, T], F32, name=f"x0_{n}") for n in range(B)]
        x0b_low = [held.tile([P, CB // 2, T], BF16, name=f"x0b_low{n}") for n in range(B)]
        x0b_high = {}

        def x0b(n, c):
            return x0b_low[n][:, c, :] if c < CB // 2 else x0b_high[n][:, c - CB // 2, :]

        def look_up(c, n):
            piece = offsets[:, n * T // 16 : (n + 1) * T // 16]
            nc.vector.tensor_tensor(
                x0[n][:, c, :], table[c][:].indirect(piece), pe_sb[:, c, :], ALU.add
            )

        def round_x0(c, n):
            if c == CB // 2:
                x0b_high[n] = seq.tile([P, CB // 2, T], BF16, name="x0b_high")
            nc.scalar.mul(x0b(n, c), x0[n][:, c, :], EMB_SCALE)

        due_next = []

        def in_next_block(step, *args):
            due_next.append((step, args))

        qkv = {}

        def new_qkv(n):
            qkv[n] = {kind: seq.tile([P, NH, T], BF16, name=kind) for kind in ("q", "k", "v")}

        def project_matmul(ps, n, kind, g, c, first=0, last=CB - 1):
            block = slice(g * P, (g + 1) * P)
            if kind == "v":
                lhsT, rhs = x0b(n, c)[:, block], weights["v"][:, c, :]
            else:
                lhsT, rhs = weights[kind][:, c, block], x0b(n, c)
            matmul(ps[:], lhsT, rhs, start=c == first, stop=c == last)

        def out_of_psum(dest, ps, kind, g):
            if kind == "q":
                nc.scalar.activation(
                    dest, ps[:], ACT.Identity, bias=bq_scaled[:, g : g + 1], scale=1.0 / math.sqrt(P)
                )
            else:
                nc.scalar.copy(dest, ps[:])

        def project_out(ps, n, kind, g):
            out_of_psum(qkv[n][kind][:, g, :], ps, kind, g)

        parked = {}

        def park_group(n, kind, g):
            ps = psum.tile([P, T], F32, name="park_ps", tag="bank")
            for c in range(PARKED_BLOCKS):
                project_matmul(ps, n, kind, g, c, last=PARKED_BLOCKS - 1)
            parked[n, kind, g] = held.tile([P, T], F32, name=f"parked_{kind}{n}{g}")
            out_of_psum(parked[n, kind, g][:], ps, kind, g)

        def parked_out(ps, n, kind, g):
            nc.vector.scalar_tensor_tensor(
                qkv[n][kind][:, g, :], ps[:], 1.0 / math.sqrt(P) if kind == "q" else 1.0,
                parked[n, kind, g][:], ALU.mult, ALU.add,
            )

        def project_group(n, kind, g):
            ps = psum.tile([P, T], F32, name="proj_ps", tag="bank")
            done = PARKED_BLOCKS if (n, kind, g) in PARKED_GROUPS else 0
            for c in range(done, CB):
                project_matmul(ps, n, kind, g, c, first=done)
            in_next_block(parked_out if done else project_out, ps, n, kind, g)

        def new_part():
            return {
                "neg_max": work.tile([P, HB], F32, name="neg_max"),
                "e": work.tile([P, HB, T], BF16, name="e"),
                "e_sum": work.tile([P, HB], F32, name="e_sum"),
            }

        def scores(n, half, h, b):
            first = half * HT + b * P
            s_ps = psum.tile([P, T], F32, name="s_ps", tag="bank")
            matmul(
                s_ps[:], qkv[n]["q"][:, h, first : first + P], qkv[n]["k"][:, h, :],
                start=True, stop=True,
            )
            return s_ps

        def exponentials(part, s_ps, tb):
            neg_max = part["neg_max"][:, tb : tb + 1]
            nc.vector.reduce_max(neg_max, s_ps[:], axis=AX.X, negate=True)
            nc.scalar.activation(
                part["e"][:, tb, :], s_ps[:], ACT.Exp, bias=neg_max, scale=1.0,
                accum_out=part["e_sum"][:, tb : tb + 1],
            )

        def normalize(part):
            recip = work.tile([P, HB], F32, name="recip")
            nc.vector.reciprocal(recip[:], part["e_sum"][:])
            for tb in range(HB):
                nc.vector.tensor_scalar_mul(
                    part["e"][:, tb, :], part["e"][:, tb, :], recip[:, tb : tb + 1]
                )

        def begin_turning(part):
            part["aT_ps"] = psum.tile([P, TB, HT], BF16, name="aT_ps", tag="bank")
            for tb in range(HB):
                for ub in range(TB):
                    to_turn.append(
                        (
                            part["aT_ps"][:, ub, tb * P : (tb + 1) * P],
                            part["e"][:, tb, ub * P : (ub + 1) * P],
                        )
                    )

        def end_turning(part):
            while to_turn:
                turn_one()
            part["aT"] = work.tile([P, TB, HT], BF16, name="aT")
            in_next_block(nc.vector.tensor_copy, part["aT"][:], part["aT_ps"][:])

        av = {}

        def weighted_sum(part, n, half, h):
            if half == 0 and h == 0:
                av[n] = seq.tile([P, NH, T], BF16, name="av")
            av_ps = psum.tile([P, HT], F32, name="av_ps", tag="bank")
            for ub in range(TB):
                matmul(
                    av_ps[:], qkv[n]["v"][:, ub, h * P : (h + 1) * P], part["aT"][:, ub, :],
                    start=ub == 0, stop=ub == TB - 1,
                )
            in_next_block(av_out, av_ps, n, half, h)

        def av_out(av_ps, n, half, h):
            nc.scalar.activation(
                av[n][:, h, half * HT : (half + 1) * HT], av_ps[:], ACT.Identity, bias=column(1, h)
            )

        norm = {}

        x0_sum = {}

        def sum_x0(n):
            pair = work.tile([P, CB // 2, T], BF16, name="pair")
            nc.vector.tensor_tensor(pair[:], x0b_low[n][:], x0b_high[n][:], ALU.add)
            x0_sum[n] = late.tile([P, T], BF16, name="x0_sum")
            nc.vector.tensor_tensor(x0_sum[n][:], pair[:, 0, :], pair[:, 1, :], ALU.add)

        def y_of(p, eb):
            n, first, blocks = PIECES[p]
            return x0[n][:, eb, first * P : (first + blocks) * P]

        def wo_step(p, eb):
            n, first, blocks = PIECES[p]
            width = blocks * P
            if eb == 0:
                norm[p] = {"sq": seq.tile([P, CB, width], BF16, name="sq")}
            y_ps = psum.tile([P, width], F32, name="y_ps", tag="bank")
            for h in range(NH):
                matmul(
                    y_ps[:], weights["o"][:, h, eb * P : (eb + 1) * P],
                    av[n][:, h, first * P : (first + blocks) * P],
                    start=h == 0, stop=False,
                )
            matmul(
                y_ps[:], minus_mean_w[:], x0_sum[n][:, first * P : (first + blocks) * P],
                start=False, stop=True,
            )
            in_next_block(residual, p, eb, y_ps)

        def residual(p, eb, y_ps):
            nc.vector.scalar_tensor_tensor(
                y_of(p, eb), y_of(p, eb), EMB_SCALE, y_ps[:], ALU.mult, ALU.add
            )
            in_next_block(square, p, eb)

        def square(p, eb):
            nc.scalar.activation(
                norm[p]["sq"][:, eb, :], y_of(p, eb), ACT.Square, bias=bo_centred[:, eb : eb + 1]
            )
            if eb == CB - 1:
                in_next_block(var_rows if p >= FIRST_LATE_PIECE else var_columns, p)

        def var_columns(p):
            blocks = PIECES[p][2]
            norm[p]["var"] = psum.tile([P, blocks], F32, name="var_cols", tag="bank")
            for b in range(blocks):
                for eb in range(CB):
                    nc.tensor.matmul(
                        norm[p]["var"][:, b : b + 1],
                        norm[p]["sq"][:, eb, b * P : (b + 1) * P], mean_w[:, 0:1],
                        start=eb == 0, stop=eb == CB - 1,
                    )
            in_next_block(rstd_columns, p)

        def rstd_columns(p):
            blocks = PIECES[p][2]
            var = work.tile([P, blocks], F32, name="var")
            nc.vector.tensor_scalar_add(var[:], norm[p]["var"][:], EPS)
            cols = work.tile([P, blocks], F32, name="rstd_cols")
            nc.gpsimd.tensor_tensor(cols[:], var[:], minus_half[:, 0:blocks], ALU.pow)
            in_next_block(rstd_rows, p, cols)

        def rstd_rows(p, cols):
            blocks = PIECES[p][2]
            norm[p]["rstd"] = psum.tile([P, blocks * P], F32, name="rstd_rows", tag="bank")
            for b in range(blocks):
                nc.tensor.transpose(
                    norm[p]["rstd"][:, b * P : (b + 1) * P],
                    cols[:, b : b + 1].to_broadcast([P, P]), ident_f[:],
                )
            in_next_block(scale_step, p)

        def var_rows(p):
            norm[p]["var"] = psum.tile([P, PIECES[p][2] * P], F32, name="var_rows", tag="bank")
            for eb in range(CB):
                matmul(
                    norm[p]["var"][:], mean_w[:], norm[p]["sq"][:, eb, :],
                    start=eb == 0, stop=eb == CB - 1,
                )
            in_next_block(rstd_step, p)

        def rstd_step(p):
            norm[p]["rstd"] = seq.tile([P, PIECES[p][2] * P], F32, name="rstd")
            nc.scalar.activation(
                norm[p]["rstd"][:], norm[p]["var"][:], ACT.Abs_reciprocal_sqrt, bias=eps_col[:]
            )
            in_next_block(scale_step, p)

        def scale_step(p):
            n, first, blocks = PIECES[p]
            for eb in range(CB):
                nc.vector.scalar_tensor_tensor(
                    y_of(p, eb), y_of(p, eb), bo_centred[:, eb : eb + 1], norm[p]["rstd"][:],
                    ALU.add, ALU.mult,
                )
            in_next_block(affine_step, p)

        def affine_step(p):
            n, first, blocks = PIECES[p]
            for eb in range(CB):
                if n < B - 2:
                    nc.vector.tensor_scalar(
                        y_of(p, eb), y_of(p, eb), column(3, eb), column(4, eb), ALU.mult, ALU.add
                    )
                else:
                    nc.scalar.activation(
                        y_of(p, eb), y_of(p, eb), ACT.Identity,
                        bias=column(4, eb), scale=column(3, eb),
                    )
                nc.sync.dma_start(
                    out[eb * P : (eb + 1) * P, n * T + first * P : n * T + (first + blocks) * P],
                    y_of(p, eb),
                )

        def finish_steps(n, blocks_done):
            return [
                (wo_step, (p, eb))
                for p, (piece_n, first, blocks) in enumerate(PIECES)
                if piece_n == n and blocks_done - HB < first + blocks <= blocks_done
                for eb in range(CB)
            ]

        def project_steps(n):
            groups = [(n, kind, g) for kind, g in V_GROUPS]
            if n == 0:
                groups = [(0, kind, g) for kind, g in QK_GROUPS[NH:]] + groups
            if n + 1 < B:
                if n + 1 not in qkv:
                    new_qkv(n + 1)
                groups += [
                    (n + 1, kind, g) for kind, g in QK_GROUPS if (n + 1, kind, g) not in OPEN_GROUPS
                ]
            return [(project_group, args) for args in groups]

        for n in range(2):
            new_qkv(n)
        open_ps = {}

        def add_to_open(n, c):
            for group in EARLY_GROUPS[n]:
                if c == 0:
                    open_ps[group] = psum.tile([P, T], F32, name="open_ps", tag="bank")
                project_matmul(open_ps[group], *group, c)

        for c in range(CB - 1):
            for n in range(B):
                look_up(c, n)
                if c < CB // 2 or n < 2:
                    round_x0(c, n)
            add_to_open(0, c)
            if c == PARKED_BLOCKS - 1:
                for group in PARKED_GROUPS:
                    park_group(*group)
        for c in range(CB - 1):
            add_to_open(1, c)
        look_up(CB - 1, 0)
        round_x0(CB - 1, 0)
        for group in OPEN_GROUPS[:2]:
            project_matmul(open_ps[group], *group, CB - 1)
            project_out(open_ps[group], *group)
        to_close = OPEN_GROUPS[2:]

        def close_group(group):
            project_matmul(open_ps[group], *group, CB - 1)
            in_next_block(project_out, open_ps[group], *group)

        parts = {}
        waiting = []
        for i in range((len(PARTS) + 3) * HB + DRAIN):
            k, b = divmod(i, HB)
            if k < len(PARTS):
                n, half, h = PARTS[k]
                if b == 0:
                    parts[k] = new_part()
                s_ps = scores(n, half, h, b)
            due = list(due_next)
            due_next.clear()
            for step, args in due:
                step(*args)
            if k < len(PARTS):
                exponentials(parts[k], s_ps, b)
            if (k, b) == (len(PARTS) - 1, HB - 1):
                early = work.tile([P, 1], F32, name="early")
                nc.scalar.activation(
                    early[:], parts[k]["e_sum"][:, b : b + 1], ACT.Abs_reciprocal_sqrt
                )
            if b == 0 and k - 1 in parts:
                normalize(parts[k - 1])
            if b == 0 and k - 2 in parts:
                begin_turning(parts[k - 2])
            if k < len(PARTS):
                j = i % BLOCKS
                if n == 0 and j + 1 < B:
                    look_up(CB - 1, j + 1)
                elif n == 0 and j + 1 == B:
                    late_bytes = last_table.tile([P, CB + 1, D], BF16, name="late_bytes", tag="bytes")
                    weights["o"] = late_bytes[:, 0:CB, :]
                    load_weights(nc.sync, "o", wo)
                    waiting.append((center_wo, ()))
                    waiting.append((center_bo, (late_bytes[:, CB, 0:CB],)))
                if j == 0:
                    ahead = project_steps(n)
                    waiting.append((sum_x0, (n,)))
                    if n + 1 < B:
                        for c in range(CB // 2 if n else CB - 1, CB):
                            round_x0(c, n + 1)
                for group in to_close[:2]:
                    close_group(group)
                to_close = to_close[2:]
                if n == 0:
                    now = ahead[j + 1 : j + 2] if j else ahead[:2]
                else:
                    now = ahead[12 * j // BLOCKS : 12 * (j + 1) // BLOCKS]
                for step, args in now:
                    step(*args)
            for turn in range(1 if k < len(PARTS) + 3 else 2):
                if waiting:
                    step, args = waiting.pop(0)
                    step(*args)
            if b == 1 and k - 3 in parts:
                n2, half2, h2 = PARTS[k - 3]
                weighted_sum(parts[k - 3], n2, half2, h2)
                if h2 == NH - 1 and n2 != B - 2:
                    in_next_block(waiting.extend, finish_steps(n2, (half2 + 1) * HB))
            if (k, b) == (len(PARTS) - 2, 0):
                waiting.extend(finish_steps(B - 2, TB))
            if b == 1 and k - 2 in parts:
                end_turning(parts[k - 2])
        assert not waiting and not due_next
